import numpy as np
import ml_dtypes


def mxq(x, axis, fmt="e4m3"):
    dtype, down = {"e4m3": (ml_dtypes.float8_e4m3fn, 7), "e5m2": (ml_dtypes.float8_e5m2, 14)}[fmt]
    v = np.moveaxis(np.asarray(x, np.float32).astype(ml_dtypes.bfloat16).astype(np.float64), axis, -1)
    blocks = v.reshape(v.shape[:-1] + (-1, 32))
    amax = np.abs(blocks).max(-1, keepdims=True)
    byte = np.maximum(np.where(amax > 0, np.frexp(amax)[1] - 1 + 127, 0) - down, 1)
    scale = np.exp2(byte - 127.0)
    codes = (blocks / scale).astype(np.float32).astype(dtype).astype(np.float64)
    return np.moveaxis((codes * scale).reshape(v.shape), -1, axis)


WIDE = False


def mx_kscale(k):
    if not WIDE:
        return np.ones(k)
    levels = np.array([10, -10, 5, -5, 0])
    if k % 512:
        return np.exp2(np.random.permutation(np.resize(levels, k // 32))).repeat(32)
    a = np.empty((k // 512, 16))
    for p in range(k // 512):
        a[p, :8] = np.random.permutation(np.resize(levels, 8))
        for g in range(8):
            far = levels[np.abs(levels - a[p, g]) >= 10]
            a[p, g + 8] = far[np.random.randint(len(far))]
    return np.exp2(a.ravel()).repeat(32)


BF16 = ml_dtypes.bfloat16


def bf(x):
    return np.asarray(x, np.float32).astype(BF16)


def f64(x):
    return np.asarray(x).astype(np.float64)


B, A, E, H, NEXP, NACT = 128, 8, 512, 512, 8, 128
M = B * A


def sigmoid(v):
    return 1.0 / (1.0 + np.exp(-v))


def setup_inputs():
    s, t = mx_kscale(H), mx_kscale(H)
    return {
        "h": bf(np.random.standard_normal((M, H)) * 0.65 * s),
        "gate_logit": bf(np.random.standard_normal((M, NEXP))),
        "e_w1": bf(np.random.standard_normal((NEXP, H, H)) * 1.5 / np.sqrt(H) / s[None, None, :] * t[None, :, None]),
        "e_b1": bf(np.random.standard_normal((NEXP, H)) * 0.3 * t[None, :]),
        "e_w2": bf(np.random.standard_normal((NEXP, NACT, H)) * 2.0 / np.sqrt(H) / t[None, None, :]),
        "e_b2": bf(np.random.standard_normal((NEXP, NACT)) * 0.3),
    }


def reference(h, gate_logit, e_w1, e_b1, e_w2, e_b2):
    hq = mxq(f64(h), 1, "e4m3")
    h1 = np.maximum((hq @ mxq(f64(e_w1), 2, "e4m3").transpose(0, 2, 1)) + f64(e_b1)[:, None, :], 0.0)
    experts_out = (mxq(h1, 2, "e4m3") @ mxq(f64(e_w2), 2, "e4m3").transpose(0, 2, 1)) + f64(e_b2)[:, None, :]
    weight = sigmoid(f64(gate_logit))
    w = weight.T[:, :, None]
    final_q = (experts_out * w).mean(axis=0)
    return final_q, np.swapaxes(experts_out, 0, 1)

@@ -1,0 +1,387 @@
+from contextlib import ExitStack
+
+import concourse.mybir as mybir
+from concourse.masks import make_identity
+
+F32 = mybir.dt.float32
+BF16 = mybir.dt.bfloat16
+U32 = mybir.dt.uint32
+U8 = mybir.dt.uint8
+FP8X4 = mybir.dt.float8_e4m3fn_x4
+ACT = mybir.ActivationFunctionType
+ALU = mybir.AluOpType
+
+P = 128
+ROWS = 1024
+H = 512
+NACT = 128
+NEXP = 8
+MT = ROWS // P
+HALF_MT = 4
+UNITS = NEXP * 2
+
+FLOPS = 2 * ROWS * H * H * NEXP + 2 * ROWS * H * NACT * NEXP
+
+PINNED = False
+S_COLS = [32, 32, 32, 32, 32, 32, 32, 32, 32, 32, 32, 32, 32, 64, 128, 256]
+V_PLANES = {}
+
+
+def tile_mspagent_pb_kernel(tc, h, gate_logit, e_w1, e_b1, e_w2, e_b2, out_0, out_1):
+    nc = tc.nc
+    with ExitStack() as ctx:
+        if PINNED:
+            ctx.enter_context(tc.manual_schedule())
+        keep = ctx.enter_context(tc.tile_pool(name="keep", bufs=1))
+        work = ctx.enter_context(tc.tile_pool(name="work", bufs=3))
+        ps_s1 = ctx.enter_context(tc.psum_pool(name="ps_s1", bufs=4))
+        ps_tp = ctx.enter_context(tc.psum_pool(name="ps_tp", bufs=2))
+        ps_s2 = ctx.enter_context(tc.psum_pool(name="ps_s2", bufs=2))
+
+        b1_rows = keep.tile([P, H], BF16, name="b1_rows")
+        nc.vector.memset(b1_rows[:], 0.0)
+        b2_rows = keep.tile([P, NEXP * NACT], BF16, name="b2_rows")
+        nc.vector.memset(b2_rows[:], 0.0)
+        gl = keep.tile([P, MT * NEXP], BF16, name="gl")
+        nc.sync.dma_start(out=gl[:], in_=gate_logit.rearrange("(p mt) x -> p (mt x)", mt=MT))
+        nc.sync.dma_start(out=b1_rows[0:NEXP, :], in_=e_b1)
+        nc.sync.dma_start(out=b2_rows[0:1, :], in_=e_b2.rearrange("(o x) a -> o (x a)", o=1))
+
+        h_view = h.rearrange("(p mt) k -> p mt k", mt=MT)
+        h_sb = []
+        w1_sb = []
+        w2_sb = []
+        for q in range(4):
+            h_tile = keep.tile([P, 2, H], BF16, name="h_sb%d" % q)
+            h_sb.append(h_tile)
+        for ex in range(NEXP):
+            for u in range(2):
+                w1_tile = keep.tile([P, 2, H], BF16, name="w1_sb%d_%d" % (ex, u))
+                w1_sb.append(w1_tile)
+        for q in range(4):
+            w2_tile = keep.tile([P, 2, H], BF16, name="w2_sb%d" % q)
+            w2_sb.append(w2_tile)
+
+        def load_h(q):
+            nc.sync.dma_start(out=h_sb[q][:], in_=h_view[:, 2 * q:2 * q + 2, :])
+
+        def load_w1(ex, u):
+            nc.sync.dma_start(
+                out=w1_sb[2 * ex + u][:], in_=e_w1[ex].rearrange("(p t) k -> p t k", t=4)[:, 2 * u:2 * u + 2, :]
+            )
+
+        def load_w2(q):
+            nc.sync.dma_start(out=w2_sb[q][:], in_=e_w2[2 * q:2 * q + 2].rearrange("x a k -> a x k"))
+
+        load_h(0)
+        load_h(1)
+        load_w1(0, 0)
+        load_w1(0, 1)
+        load_h(2)
+        load_h(3)
+        load_w1(1, 0)
+        load_w1(1, 1)
+        load_w2(0)
+        load_w1(2, 0)
+        load_w1(2, 1)
+        load_w2(1)
+        load_w1(3, 0)
+        load_w1(3, 1)
+        load_w2(2)
+        load_w1(4, 0)
+        load_w1(4, 1)
+        load_w2(3)
+        for ex in range(5, NEXP):
+            load_w1(ex, 0)
+            load_w1(ex, 1)
+
+        ident = keep.tile([P, P], F32, name="ident")
+        make_identity(nc, ident[:])
+        ones = keep.tile([P, P], BF16, name="ones")
+        nc.vector.memset(ones[:], 1.0)
+
+        gate = keep.tile([P, MT * NEXP], F32, name="gate")
+        nc.scalar.activation(out=gate[:], in_=gl[:], func=ACT.Sigmoid)
+        nc.vector.tensor_scalar(out=gate[:], in0=gate[:], scalar1=1.0 / NEXP, scalar2=None, op0=ALU.mult)
+
+        b1_bank = ps_s2.tile([P, 512], F32, name="b1_bank", tag="s2")
+        b1T = keep.tile([P, 4 * NEXP], F32, name="b1T")
+        for u in range(2):
+            nc.tensor.transpose(b1_bank[:, u * P:(u + 1) * P], b1_rows[:].bitcast(F32)[:, u:2 * P:2], ident[:])
+            nc.vector.tensor_copy(
+                out=b1T[:].rearrange("p (x u e) -> p x u e", u=2, e=2)[:, :, u, :],
+                in_=b1_bank[:, u * P:(u + 1) * P].bitcast(BF16)[:, 0:2 * NEXP].rearrange("p (x e) -> p x e", e=2),
+            )
+
+        b2bc = keep.tile([P, NEXP * NACT], F32, name="b2bc")
+
+        def spread_b2(c, engine):
+            b2_bank = ps_s2.tile([P, 512], F32, name="b2_bank", tag="s2")
+            nc.tensor.matmul(out=b2_bank[:], lhsT=ones[:], rhs=b2_rows[:, c * 512:(c + 1) * 512], start=True, stop=True)
+            if engine == "v":
+                nc.vector.tensor_copy(out=b2bc[:, c * 512:(c + 1) * 512], in_=b2_bank[:])
+            else:
+                nc.scalar.copy(out=b2bc[:, c * 512:(c + 1) * 512], in_=b2_bank[:])
+
+        def t_bank(src_tile, pool_tag):
+            if pool_tag == "s1":
+                bank = ps_s1.tile([P, 2, 2, P], F32, name="tp_bank1", tag="s1")
+            else:
+                bank = ps_tp.tile([P, 2, 2, P], F32, name="tp_bank", tag="tp")
+            for s in range(2):
+                words = src_tile[:, s, :].bitcast(F32)
+                for u in range(2):
+                    nc.tensor.transpose(bank[:, s, u, :], words[:, u:2 * P:2], ident[:])
+            return bank
+
+        def x_bank(bank, grouped, engine):
+            dst = grouped.bitcast(F32).rearrange("p (s c u) -> p s c u", s=2, u=2)
+            src = bank[:].rearrange("p s u c -> p s c u")
+            if engine == "v":
+                nc.vector.tensor_copy(out=dst, in_=src)
+            else:
+                nc.scalar.copy(out=dst, in_=src)
+
+        def quantise(grouped, codes, scales):
+            nc.vector.quantize_mx(out=codes.bitcast(FP8X4), scales=scales, in_=grouped)
+
+        grp = {}
+        cod = {}
+        sca = {}
+        for half in range(2):
+            g_tile = keep.tile([P, 512 * 4], BF16, name="h_g%d" % half, align_bytes=64)
+            c_tile = keep.tile([P, 512], U32, name="h_c%d" % half, align_bytes=64)
+            s_tile = keep.tile([P, 512], U8, name="h_s%d" % half, align_bytes=64)
+            grp[("h", half)] = g_tile
+            cod[("h", half)] = c_tile
+            sca[("h", half)] = s_tile
+        for ex in range(NEXP):
+            c_tile = keep.tile([P, 512], U32, name="w1_c%d" % ex, align_bytes=64)
+            s_tile = keep.tile([P, 512], U8, name="w1_s%d" % ex, align_bytes=64)
+            cod[("w1", ex)] = c_tile
+            sca[("w1", ex)] = s_tile
+        for q in range(4):
+            c_tile = keep.tile([P, 256], U32, name="w2_c%d" % q, align_bytes=64)
+            s_tile = keep.tile([P, 256], U8, name="w2_s%d" % q, align_bytes=64)
+            cod[("w2", q)] = c_tile
+            sca[("w2", q)] = s_tile
+        live_banks = {}
+
+        def job_t(kind, idx, b, pool_tag="tp"):
+            if kind == "w1" and b == 0:
+                g_tile = work.tile([P, 512 * 4], BF16, name="w1_g", tag="w1_g", align_bytes=64)
+                grp[(kind, idx)] = g_tile
+            if kind == "w2":
+                g_tile = work.tile([P, 256 * 4], BF16, name="w2_g", tag="w2_g", bufs=2, align_bytes=64)
+                grp[(kind, idx)] = g_tile
+            if kind == "h":
+                src_tile = h_sb[2 * idx + b]
+            elif kind == "w1":
+                src_tile = w1_sb[2 * idx + b]
+            else:
+                src_tile = w2_sb[idx]
+            live_banks[(kind, idx, b)] = t_bank(src_tile, pool_tag)
+
+        def job_x(kind, idx, b, engine):
+            x_bank(live_banks[(kind, idx, b)], grp[(kind, idx)][:, b * 1024:(b + 1) * 1024], engine)
+
+        def job_q(kind, idx, lo=0, hi=None):
+            width = cod[(kind, idx)].shape[1]
+            top = width if hi is None else hi
+            quantise(grp[(kind, idx)][:, 4 * lo:4 * top], cod[(kind, idx)][:, lo:top], sca[(kind, idx)][:, lo:top])
+
+        s1_banks = {}
+        planes = {}
+        h1_g = {}
+        h1_c = {}
+        h1_s = {}
+        s2_bank = {}
+        y_sb = {}
+        acc = []
+        for half in range(2):
+            acc_tile = keep.tile([P, HALF_MT, NACT], F32, name="acc%d" % half)
+            acc.append(acc_tile)
+        out1_view = out_1.rearrange("(p mt) x a -> p mt x a", mt=MT)
+        out0_view = out_0.rearrange("(p mt) a -> p mt a", mt=MT)
+
+        def mm1(n, ts=(0, 1, 2, 3)):
+            ex, half = n // 2, n % 2
+            if n not in s1_banks:
+                s1_banks[n] = {}
+                pl_tile = work.tile([P, 4, 512], BF16, name="planes", tag="planes")
+                planes[n] = pl_tile
+            for t in ts:
+                bank = ps_s1.tile([P, 512], F32, name="s1_bank", tag="s1")
+                nc.tensor.matmul_mx(
+                    out=bank[:],
+                    lhsT=cod[("w1", ex)][:, t * P:(t + 1) * P].bitcast(FP8X4),
+                    lhsT_scale=sca[("w1", ex)][:, t * P:(t + 1) * P],
+                    rhs=cod[("h", half)][:].bitcast(FP8X4),
+                    rhs_scale=sca[("h", half)][:],
+                    start=True,
+                    stop=True,
+                )
+                s1_banks[n][t] = bank
+
+        def c1(n, t):
+            ex = n // 2
+            bias = b1T[:, 4 * ex + t:4 * ex + t + 1]
+            if t in V_PLANES.get(n, ()):
+                nc.vector.tensor_scalar(
+                    out=planes[n][:, t, :], in0=s1_banks[n][t][:], scalar1=bias, scalar2=0.0, op0=ALU.add, op1=ALU.max
+                )
+            else:
+                nc.scalar.activation(out=planes[n][:, t, :], in_=s1_banks[n][t][:], func=ACT.Relu, bias=bias, scale=1.0)
+
+        def regroup(n, engine):
+            if n not in h1_g:
+                g_tile = work.tile([P, 512 * 4], BF16, name="h1_g", tag="h1_g", align_bytes=64)
+                h1_g[n] = g_tile
+            cut = 512 - S_COLS[n]
+            lo, hi = (0, cut) if engine == "v" else (cut, 512)
+            if lo == hi:
+                return
+            dst = h1_g[n][:, 4 * lo:4 * hi].rearrange("p (c i t) -> p c t i", i=4, t=4)
+            src = planes[n][:, :, lo:hi].rearrange("p t (c i) -> p c t i", i=4)
+            if engine == "v":
+                nc.vector.tensor_copy(out=dst, in_=src)
+            else:
+                nc.scalar.copy(out=dst, in_=src)
+
+        def q1(n, lo=0, hi=512):
+            if n not in h1_c:
+                c_tile = work.tile([P, 512], U32, name="h1_c", tag="h1_c", align_bytes=64)
+                s_tile = work.tile([P, 512], U8, name="h1_s", tag="h1_s", align_bytes=64)
+                h1_c[n] = c_tile
+                h1_s[n] = s_tile
+            quantise(h1_g[n][:, 4 * lo:4 * hi], h1_c[n][:, lo:hi], h1_s[n][:, lo:hi])
+
+        def mm2(n, tiles=(0, 1, 2, 3)):
+            ex = n // 2
+            if n not in s2_bank:
+                bank = ps_s2.tile([P, HALF_MT, NACT], F32, name="s2_bank", tag="s2")
+                s2_bank[n] = bank
+            lo = (ex % 2) * NACT
+            for i in tiles:
+                nc.tensor.matmul_mx(
+                    out=s2_bank[n][:, i, :],
+                    lhsT=h1_c[n][:, i * P:(i + 1) * P].bitcast(FP8X4),
+                    lhsT_scale=h1_s[n][:, i * P:(i + 1) * P],
+                    rhs=cod[("w2", ex // 2)][:, lo:lo + NACT].bitcast(FP8X4),
+                    rhs_scale=sca[("w2", ex // 2)][:, lo:lo + NACT],
+                    start=True,
+                    stop=True,
+                )
+
+        def add_b2(n):
+            ex = n // 2
+            y_tile = work.tile([P, HALF_MT, NACT], F32, name="y_sb", tag="y_sb", bufs=4)
+            y_sb[n] = y_tile
+            nc.vector.tensor_tensor(
+                out=y_tile[:],
+                in0=s2_bank[n][:],
+                in1=b2bc[:, ex * NACT:(ex + 1) * NACT].unsqueeze(1).to_broadcast([P, HALF_MT, NACT]),
+                op=ALU.add,
+            )
+
+        def gate_sum(n):
+            ex, half = n // 2, n % 2
+            for i in range(HALF_MT):
+                col = (half * HALF_MT + i) * NEXP + ex
+                if ex == 0:
+                    nc.vector.tensor_scalar(
+                        out=acc[half][:, i, :], in0=y_sb[n][:, i, :], scalar1=gate[:, col:col + 1], scalar2=None, op0=ALU.mult
+                    )
+                else:
+                    nc.vector.scalar_tensor_tensor(
+                        out=acc[half][:, i, :],
+                        in0=y_sb[n][:, i, :],
+                        scalar=gate[:, col:col + 1],
+                        in1=acc[half][:, i, :],
+                        op0=ALU.mult,
+                        op1=ALU.add,
+                    )
+
+        def store(n):
+            ex, half = n // 2, n % 2
+            nc.sync.dma_start(out=out1_view[:, half * HALF_MT:(half + 1) * HALF_MT, ex, :], in_=y_sb[n][:])
+            if ex == NEXP - 1:
+                nc.sync.dma_start(out=out0_view[:, half * HALF_MT:(half + 1) * HALF_MT, :], in_=acc[half][:])
+
+        job_t("h", 0, 0)
+        job_t("h", 0, 1)
+        job_x("h", 0, 0, "v")
+        job_x("h", 0, 1, "s")
+        job_t("w1", 0, 0)
+        job_t("w1", 0, 1)
+        job_q("h", 0, 0, 256)
+        job_x("w1", 0, 0, "v")
+        job_x("w1", 0, 1, "s")
+        job_q("h", 0, 256, 512)
+        job_q("w1", 0, 0, 256)
+        job_q("w1", 0, 256, 512)
+        job_t("h", 1, 0)
+        mm1(0, (0, 1))
+        job_t("h", 1, 1)
+        mm1(0, (2, 3))
+        job_x("h", 1, 0, "v")
+        job_x("h", 1, 1, "v")
+        job_q("h", 1)
+        for t in range(4):
+            c1(0, t)
+        regroup(0, "s")
+        job_t("w1", 1, 0)
+        job_t("w1", 1, 1)
+        job_x("w1", 1, 0, "v")
+        job_x("w1", 1, 1, "v")
+
+        prep_plan = {
+            1: [("b2", 0, "ss")],
+            2: [("w1", 2, "ss")],
+            3: [("w2", 1, "s")],
+            4: [("w1", 3, "ss")],
+            5: [("w2", 2, "s")],
+            6: [("w1", 4, "ss")],
+            7: [("w2", 3, "s")],
+            8: [("w1", 5, "ss")],
+            10: [("w1", 6, "ss")],
+            12: [("w1", 7, "ss")],
+        }
+
+        for k in range(1, UNITS + 2):
+            jobs = prep_plan.get(k, [])
+            if k < UNITS:
+                mm1(k)
+            if k >= 2:
+                mm2(k - 2)
+            if k < UNITS:
+                for t in range(4):
+                    c1(k, t)
+                regroup(k, "s")
+            for kind, idx, engines in jobs:
+                if kind == "b2":
+                    spread_b2(0, engines[0])
+                    spread_b2(1, engines[1])
+                else:
+                    for b in range(len(engines)):
+                        job_t(kind, idx, b)
+                    for b in range(len(engines)):
+                        job_x(kind, idx, b, engines[b])
+            if 1 <= k <= UNITS:
+                regroup(k - 1, "v")
+            if k == 1:
+                job_q("w1", 1)
+                job_t("w2", 0, 0)
+                job_x("w2", 0, 0, "v")
+            for kind, idx, engines in prep_plan.get(k - 1, []):
+                if kind != "b2":
+                    job_q(kind, idx)
+            if k >= 2:
+                add_b2(k - 2)
+            if 1 <= k <= UNITS:
+                q1(k - 1)
+            if k == 1:
+                job_q("w2", 0)
+            if k >= 2:
+                gate_sum(k - 2)
+                store(k - 2)

@@ -22,30 +22,32 @@ UNITS = NEXP * 2
 
 FLOPS = 2 * ROWS * H * H * NEXP + 2 * ROWS * H * NACT * NEXP
 
-PINNED = False
-S_COLS = [32, 32, 32, 32, 32, 32, 32, 32, 32, 32, 32, 32, 32, 64, 128, 256]
-V_PLANES = {}
+S_COLS = [0] * 12 + [32, 64, 96]
+S_LAST = 256
 
 
 def tile_mspagent_pb_kernel(tc, h, gate_logit, e_w1, e_b1, e_w2, e_b2, out_0, out_1):
     nc = tc.nc
     with ExitStack() as ctx:
-        if PINNED:
-            ctx.enter_context(tc.manual_schedule())
+        ctx.enter_context(tc.manual_schedule())
         keep = ctx.enter_context(tc.tile_pool(name="keep", bufs=1))
         work = ctx.enter_context(tc.tile_pool(name="work", bufs=3))
         ps_s1 = ctx.enter_context(tc.psum_pool(name="ps_s1", bufs=4))
         ps_tp = ctx.enter_context(tc.psum_pool(name="ps_tp", bufs=2))
         ps_s2 = ctx.enter_context(tc.psum_pool(name="ps_s2", bufs=2))
 
+        ident = keep.tile([P, P], F32, name="ident")
+        make_identity(nc, ident[:])
         b1_rows = keep.tile([P, H], BF16, name="b1_rows")
-        nc.vector.memset(b1_rows[:], 0.0)
-        b2_rows = keep.tile([P, NEXP * NACT], BF16, name="b2_rows")
-        nc.vector.memset(b2_rows[:], 0.0)
+        nc.vector.memset(b1_rows[:].bitcast(F32), 0.0)
+        b2_row = keep.tile([P, NEXP * NACT], BF16, name="b2_row")
+        nc.vector.memset(b2_row[:].bitcast(F32), 0.0)
+        ones = keep.tile([P, P], BF16, name="ones")
+        nc.vector.memset(ones[:], 1.0)
+        gate = keep.tile([P, MT * NEXP], F32, name="gate")
+
         gl = keep.tile([P, MT * NEXP], BF16, name="gl")
         nc.sync.dma_start(out=gl[:], in_=gate_logit.rearrange("(p mt) x -> p (mt x)", mt=MT))
-        nc.sync.dma_start(out=b1_rows[0:NEXP, :], in_=e_b1)
-        nc.sync.dma_start(out=b2_rows[0:1, :], in_=e_b2.rearrange("(o x) a -> o (x a)", o=1))
 
         h_view = h.rearrange("(p mt) k -> p mt k", mt=MT)
         h_sb = []
@@ -74,9 +76,11 @@ def tile_mspagent_pb_kernel(tc, h, gate_logit, e_w1, e_b1, e_w2, e_b2, out_0, ou
             nc.sync.dma_start(out=w2_sb[q][:], in_=e_w2[2 * q:2 * q + 2].rearrange("x a k -> a x k"))
 
         load_h(0)
+        nc.sync.dma_start(out=b1_rows[0:NEXP, :], in_=e_b1)
         load_h(1)
         load_w1(0, 0)
         load_w1(0, 1)
+        nc.sync.dma_start(out=b2_row[0:1, :], in_=e_b2.rearrange("(o x) a -> o (x a)", o=1))
         load_h(2)
         load_h(3)
         load_w1(1, 0)
@@ -95,33 +99,7 @@ def tile_mspagent_pb_kernel(tc, h, gate_logit, e_w1, e_b1, e_w2, e_b2, out_0, ou
             load_w1(ex, 0)
             load_w1(ex, 1)
 
-        ident = keep.tile([P, P], F32, name="ident")
-        make_identity(nc, ident[:])
-        ones = keep.tile([P, P], BF16, name="ones")
-        nc.vector.memset(ones[:], 1.0)
-
-        gate = keep.tile([P, MT * NEXP], F32, name="gate")
         nc.scalar.activation(out=gate[:], in_=gl[:], func=ACT.Sigmoid)
-        nc.vector.tensor_scalar(out=gate[:], in0=gate[:], scalar1=1.0 / NEXP, scalar2=None, op0=ALU.mult)
-
-        b1_bank = ps_s2.tile([P, 512], F32, name="b1_bank", tag="s2")
-        b1T = keep.tile([P, 4 * NEXP], F32, name="b1T")
-        for u in range(2):
-            nc.tensor.transpose(b1_bank[:, u * P:(u + 1) * P], b1_rows[:].bitcast(F32)[:, u:2 * P:2], ident[:])
-            nc.vector.tensor_copy(
-                out=b1T[:].rearrange("p (x u e) -> p x u e", u=2, e=2)[:, :, u, :],
-                in_=b1_bank[:, u * P:(u + 1) * P].bitcast(BF16)[:, 0:2 * NEXP].rearrange("p (x e) -> p x e", e=2),
-            )
-
-        b2bc = keep.tile([P, NEXP * NACT], F32, name="b2bc")
-
-        def spread_b2(c, engine):
-            b2_bank = ps_s2.tile([P, 512], F32, name="b2_bank", tag="s2")
-            nc.tensor.matmul(out=b2_bank[:], lhsT=ones[:], rhs=b2_rows[:, c * 512:(c + 1) * 512], start=True, stop=True)
-            if engine == "v":
-                nc.vector.tensor_copy(out=b2bc[:, c * 512:(c + 1) * 512], in_=b2_bank[:])
-            else:
-                nc.scalar.copy(out=b2bc[:, c * 512:(c + 1) * 512], in_=b2_bank[:])
 
         def t_bank(src_tile, pool_tag):
             if pool_tag == "s1":
@@ -223,24 +201,19 @@ def tile_mspagent_pb_kernel(tc, h, gate_logit, e_w1, e_b1, e_w2, e_b2, out_0, ou
                 )
                 s1_banks[n][t] = bank
 
-        def c1(n, t):
+        def c1(n, t, lo=0, hi=512):
             ex = n // 2
             bias = b1T[:, 4 * ex + t:4 * ex + t + 1]
-            if t in V_PLANES.get(n, ()):
-                nc.vector.tensor_scalar(
-                    out=planes[n][:, t, :], in0=s1_banks[n][t][:], scalar1=bias, scalar2=0.0, op0=ALU.add, op1=ALU.max
-                )
-            else:
-                nc.scalar.activation(out=planes[n][:, t, :], in_=s1_banks[n][t][:], func=ACT.Relu, bias=bias, scale=1.0)
+            nc.scalar.activation(
+                out=planes[n][:, t, lo:hi], in_=s1_banks[n][t][:, lo:hi], func=ACT.Relu, bias=bias, scale=1.0
+            )
 
-        def regroup(n, engine):
+        def regroup(n, engine, lo, hi):
+            if lo == hi:
+                return
             if n not in h1_g:
                 g_tile = work.tile([P, 512 * 4], BF16, name="h1_g", tag="h1_g", align_bytes=64)
                 h1_g[n] = g_tile
-            cut = 512 - S_COLS[n]
-            lo, hi = (0, cut) if engine == "v" else (cut, 512)
-            if lo == hi:
-                return
             dst = h1_g[n][:, 4 * lo:4 * hi].rearrange("p (c i t) -> p c t i", i=4, t=4)
             src = planes[n][:, :, lo:hi].rearrange("p t (c i) -> p c t i", i=4)
             if engine == "v":
@@ -258,13 +231,12 @@ def tile_mspagent_pb_kernel(tc, h, gate_logit, e_w1, e_b1, e_w2, e_b2, out_0, ou
 
         def mm2(n, tiles=(0, 1, 2, 3)):
             ex = n // 2
-            if n not in s2_bank:
-                bank = ps_s2.tile([P, HALF_MT, NACT], F32, name="s2_bank", tag="s2")
-                s2_bank[n] = bank
+            bank = ps_s2.tile([P, HALF_MT, NACT], F32, name="s2_bank", tag="s2")
             lo = (ex % 2) * NACT
             for i in tiles:
+                s2_bank[(n, i)] = bank
                 nc.tensor.matmul_mx(
-                    out=s2_bank[n][:, i, :],
+                    out=bank[:, i, :],
                     lhsT=h1_c[n][:, i * P:(i + 1) * P].bitcast(FP8X4),
                     lhsT_scale=h1_s[n][:, i * P:(i + 1) * P],
                     rhs=cod[("w2", ex // 2)][:, lo:lo + NACT].bitcast(FP8X4),
@@ -273,20 +245,21 @@ def tile_mspagent_pb_kernel(tc, h, gate_logit, e_w1, e_b1, e_w2, e_b2, out_0, ou
                     stop=True,
                 )
 
-        def add_b2(n):
+        def add_b2(n, lo=0, hi=HALF_MT):
             ex = n // 2
-            y_tile = work.tile([P, HALF_MT, NACT], F32, name="y_sb", tag="y_sb", bufs=4)
-            y_sb[n] = y_tile
+            if n not in y_sb:
+                y_tile = work.tile([P, HALF_MT, NACT], F32, name="y_sb", tag="y_sb", bufs=4)
+                y_sb[n] = y_tile
             nc.vector.tensor_tensor(
-                out=y_tile[:],
-                in0=s2_bank[n][:],
-                in1=b2bc[:, ex * NACT:(ex + 1) * NACT].unsqueeze(1).to_broadcast([P, HALF_MT, NACT]),
+                out=y_sb[n][:, lo:hi, :],
+                in0=s2_bank[(n, lo)][:, lo:hi, :],
+                in1=b2bc[:, ex * NACT:(ex + 1) * NACT].unsqueeze(1).to_broadcast([P, hi - lo, NACT]),
                 op=ALU.add,
             )
 
-        def gate_sum(n):
+        def gate_sum(n, lo=0, hi=HALF_MT):
             ex, half = n // 2, n % 2
-            for i in range(HALF_MT):
+            for i in range(lo, hi):
                 col = (half * HALF_MT + i) * NEXP + ex
                 if ex == 0:
                     nc.vector.tensor_scalar(
@@ -302,86 +275,120 @@ def tile_mspagent_pb_kernel(tc, h, gate_logit, e_w1, e_b1, e_w2, e_b2, out_0, ou
                         op1=ALU.add,
                     )
 
-        def store(n):
+        def store(n, lo=0, hi=HALF_MT):
             ex, half = n // 2, n % 2
-            nc.sync.dma_start(out=out1_view[:, half * HALF_MT:(half + 1) * HALF_MT, ex, :], in_=y_sb[n][:])
+            a, b = half * HALF_MT + lo, half * HALF_MT + hi
+            nc.sync.dma_start(out=out1_view[:, a:b, ex, :], in_=y_sb[n][:, lo:hi, :])
             if ex == NEXP - 1:
-                nc.sync.dma_start(out=out0_view[:, half * HALF_MT:(half + 1) * HALF_MT, :], in_=acc[half][:])
+                nc.sync.dma_start(out=out0_view[:, a:b, :], in_=acc[half][:, lo:hi, :])
 
         job_t("h", 0, 0)
         job_t("h", 0, 1)
+        b1_bank = ps_s2.tile([P, 512], F32, name="b1_bank", tag="s2")
+        b1T = keep.tile([P, 4 * NEXP], F32, name="b1T")
+        for u in range(2):
+            nc.tensor.transpose(b1_bank[:, u * P:(u + 1) * P], b1_rows[:].bitcast(F32)[:, u:2 * P:2], ident[:])
+        for u in range(2):
+            nc.scalar.copy(
+                out=b1T[:].rearrange("p (x u e) -> p x u e", u=2, e=2)[:, :, u, :],
+                in_=b1_bank[:, u * P:(u + 1) * P].bitcast(BF16)[:, 0:2 * NEXP].rearrange("p (x e) -> p x e", e=2),
+            )
+
+        job_t("w1", 0, 0, "s1")
+        job_t("w1", 0, 1, "s1")
         job_x("h", 0, 0, "v")
         job_x("h", 0, 1, "s")
-        job_t("w1", 0, 0)
-        job_t("w1", 0, 1)
         job_q("h", 0, 0, 256)
-        job_x("w1", 0, 0, "v")
-        job_x("w1", 0, 1, "s")
+        job_x("w1", 0, 0, "s")
+        b2bc = keep.tile([P, NEXP * NACT], F32, name="b2bc")
+        for c in range(2):
+            b2_bank = ps_s2.tile([P, 512], F32, name="b2_bank", tag="s2")
+            nc.tensor.matmul(out=b2_bank[:], lhsT=ones[:], rhs=b2_row[:, c * 512:(c + 1) * 512], start=True, stop=True)
+            nc.scalar.copy(out=b2bc[:, c * 512:(c + 1) * 512], in_=b2_bank[:])
         job_q("h", 0, 256, 512)
         job_q("w1", 0, 0, 256)
-        job_q("w1", 0, 256, 512)
+        job_x("w1", 0, 1, "v")
         job_t("h", 1, 0)
+        job_x("h", 1, 0, "v")
+        job_q("w1", 0, 256, 512)
+
         mm1(0, (0, 1))
         job_t("h", 1, 1)
         mm1(0, (2, 3))
-        job_x("h", 1, 0, "v")
         job_x("h", 1, 1, "v")
-        job_q("h", 1)
         for t in range(4):
             c1(0, t)
-        regroup(0, "s")
         job_t("w1", 1, 0)
         job_t("w1", 1, 1)
         job_x("w1", 1, 0, "v")
+        job_q("h", 1)
         job_x("w1", 1, 1, "v")
+        job_t("w2", 0, 0)
+        job_x("w2", 0, 0, "s")
 
         prep_plan = {
-            1: [("b2", 0, "ss")],
-            2: [("w1", 2, "ss")],
-            3: [("w2", 1, "s")],
-            4: [("w1", 3, "ss")],
-            5: [("w2", 2, "s")],
-            6: [("w1", 4, "ss")],
-            7: [("w2", 3, "s")],
-            8: [("w1", 5, "ss")],
-            10: [("w1", 6, "ss")],
-            12: [("w1", 7, "ss")],
+            0: ("w1", 2, "ss"),
+            1: ("w2", 1, "s"),
+            2: ("w1", 3, "ss"),
+            3: ("w1", 4, "ss"),
+            5: ("w2", 2, "s"),
+            6: ("w1", 5, "ss"),
+            7: ("w1", 6, "ss"),
+            9: ("w2", 3, "s"),
+            10: ("w1", 7, "ss"),
         }
 
-        for k in range(1, UNITS + 2):
-            jobs = prep_plan.get(k, [])
-            if k < UNITS:
-                mm1(k)
-            if k >= 2:
-                mm2(k - 2)
-            if k < UNITS:
+        nc.vector.tensor_scalar(out=gate[:], in0=gate[:], scalar1=1.0 / NEXP, scalar2=None, op0=ALU.mult)
+        LAST = UNITS - 1
+        for k in range(LAST):
+            mm1(k + 1)
+            if k >= 1:
+                mm2(k - 1)
+            if k + 1 < LAST:
                 for t in range(4):
-                    c1(k, t)
-                regroup(k, "s")
-            for kind, idx, engines in jobs:
-                if kind == "b2":
-                    spread_b2(0, engines[0])
-                    spread_b2(1, engines[1])
-                else:
-                    for b in range(len(engines)):
-                        job_t(kind, idx, b)
-                    for b in range(len(engines)):
-                        job_x(kind, idx, b, engines[b])
-            if 1 <= k <= UNITS:
-                regroup(k - 1, "v")
-            if k == 1:
+                    c1(k + 1, t)
+            else:
+                for lo in (0, 256):
+                    for t in range(4):
+                        c1(LAST, t, lo, lo + 256)
+            regroup(k, "s", 512 - S_COLS[k], 512)
+            job = prep_plan.get(k)
+            if job:
+                for b in range(len(job[2])):
+                    job_t(job[0], job[1], b)
+                for b in range(len(job[2])):
+                    job_x(job[0], job[1], b, job[2][b])
+            regroup(k, "v", 0, 512 - S_COLS[k])
+            if k == 0:
                 job_q("w1", 1)
-                job_t("w2", 0, 0)
-                job_x("w2", 0, 0, "v")
-            for kind, idx, engines in prep_plan.get(k - 1, []):
-                if kind != "b2":
-                    job_q(kind, idx)
-            if k >= 2:
-                add_b2(k - 2)
-            if 1 <= k <= UNITS:
-                q1(k - 1)
-            if k == 1:
+            job = prep_plan.get(k - 1)
+            if job:
+                job_q(job[0], job[1])
+            if k >= 1:
+                add_b2(k - 1)
+            q1(k)
+            if k >= 1:
+                gate_sum(k - 1)
+                store(k - 1)
+            else:
                 job_q("w2", 0)
-            if k >= 2:
-                gate_sum(k - 2)
-                store(k - 2)
+
+        mm2(LAST - 1)
+        regroup(LAST, "s", 256 - S_LAST, 256)
+        regroup(LAST, "s", 512 - S_LAST, 512)
+        regroup(LAST, "v", 0, 256 - S_LAST)
+        add_b2(LAST - 1)
+        q1(LAST, 0, 256)
+        mm2(LAST, (0, 1))
+        regroup(LAST, "v", 256, 512 - S_LAST)
+        gate_sum(LAST - 1, 0, 2)
+        q1(LAST, 256, 512)
+        mm2(LAST, (2, 3))
+        gate_sum(LAST - 1, 2, 4)
+        store(LAST - 1)
+        add_b2(LAST, 0, 2)
+        add_b2(LAST, 2, 4)
+        gate_sum(LAST, 0, 2)
+        store(LAST, 0, 2)
+        gate_sum(LAST, 2, 4)
+        store(LAST, 2, 4)

@@ -38,12 +38,12 @@ def tile_mspagent_pb_kernel(tc, h, gate_logit, e_w1, e_b1, e_w2, e_b2, out_0, ou
 
         ident = keep.tile([P, P], F32, name="ident")
         make_identity(nc, ident[:])
+        ones = keep.tile([P, 512], BF16, name="ones")
+        nc.vector.memset(ones[:], 1.0)
         b1_rows = keep.tile([P, H], BF16, name="b1_rows")
         nc.vector.memset(b1_rows[:].bitcast(F32), 0.0)
         b2_row = keep.tile([P, NEXP * NACT], BF16, name="b2_row")
         nc.vector.memset(b2_row[:].bitcast(F32), 0.0)
-        ones = keep.tile([P, P], BF16, name="ones")
-        nc.vector.memset(ones[:], 1.0)
         gate = keep.tile([P, MT * NEXP], F32, name="gate")
 
         gl = keep.tile([P, MT * NEXP], BF16, name="gl")
@@ -282,8 +282,15 @@ def tile_mspagent_pb_kernel(tc, h, gate_logit, e_w1, e_b1, e_w2, e_b2, out_0, ou
             if ex == NEXP - 1:
                 nc.sync.dma_start(out=out0_view[:, a:b, :], in_=acc[half][:, lo:hi, :])
 
+        def warm_up(count):
+            warm_bank = ps_s2.tile([P, 512], F32, name="warm_bank", tag="s2")
+            for i in range(count):
+                nc.tensor.matmul(out=warm_bank[:], lhsT=ones[:, 0:P], rhs=ones[:], start=True, stop=True)
+
+        warm_up(5)
         job_t("h", 0, 0)
         job_t("h", 0, 1)
+        warm_up(1)
         b1_bank = ps_s2.tile([P, 512], F32, name="b1_bank", tag="s2")
         b1T = keep.tile([P, 4 * NEXP], F32, name="b1T")
         for u in range(2):
@@ -303,7 +310,7 @@ def tile_mspagent_pb_kernel(tc, h, gate_logit, e_w1, e_b1, e_w2, e_b2, out_0, ou
         b2bc = keep.tile([P, NEXP * NACT], F32, name="b2bc")
         for c in range(2):
             b2_bank = ps_s2.tile([P, 512], F32, name="b2_bank", tag="s2")
-            nc.tensor.matmul(out=b2_bank[:], lhsT=ones[:], rhs=b2_row[:, c * 512:(c + 1) * 512], start=True, stop=True)
+            nc.tensor.matmul(out=b2_bank[:], lhsT=ones[:, 0:P], rhs=b2_row[:, c * 512:(c + 1) * 512], start=True, stop=True)
             nc.scalar.copy(out=b2bc[:, c * 512:(c + 1) * 512], in_=b2_bank[:])
         job_q("h", 0, 256, 512)
         job_q("w1", 0, 0, 256)

@@ -22,7 +22,7 @@ UNITS = NEXP * 2
 
 FLOPS = 2 * ROWS * H * H * NEXP + 2 * ROWS * H * NACT * NEXP
 
-S_COLS = [0] * 12 + [32, 64, 96]
+S_COLS = [0] * 9 + [64] * 4 + [96, 128]
 S_LAST = 256
 
 
@@ -42,11 +42,11 @@ def tile_mspagent_pb_kernel(tc, h, gate_logit, e_w1, e_b1, e_w2, e_b2, out_0, ou
         nc.vector.memset(ones[:], 1.0)
         b1_rows = keep.tile([P, H], BF16, name="b1_rows")
         nc.vector.memset(b1_rows[:].bitcast(F32), 0.0)
-        b2_row = keep.tile([P, NEXP * NACT], BF16, name="b2_row")
-        nc.vector.memset(b2_row[:].bitcast(F32), 0.0)
+        b2bc = keep.tile([P, NEXP * NACT], BF16, name="b2bc")
         gate = keep.tile([P, MT * NEXP], F32, name="gate")
 
         gl = keep.tile([P, MT * NEXP], BF16, name="gl")
+        nc.sync.dma_start(out=b1_rows[0:NEXP, :], in_=e_b1)
         nc.sync.dma_start(out=gl[:], in_=gate_logit.rearrange("(p mt) x -> p (mt x)", mt=MT))
 
         h_view = h.rearrange("(p mt) k -> p mt k", mt=MT)
@@ -76,11 +76,9 @@ def tile_mspagent_pb_kernel(tc, h, gate_logit, e_w1, e_b1, e_w2, e_b2, out_0, ou
             nc.sync.dma_start(out=w2_sb[q][:], in_=e_w2[2 * q:2 * q + 2].rearrange("x a k -> a x k"))
 
         load_h(0)
-        nc.sync.dma_start(out=b1_rows[0:NEXP, :], in_=e_b1)
-        load_h(1)
         load_w1(0, 0)
+        load_h(1)
         load_w1(0, 1)
-        nc.sync.dma_start(out=b2_row[0:1, :], in_=e_b2.rearrange("(o x) a -> o (x a)", o=1))
         load_h(2)
         load_h(3)
         load_w1(1, 0)
@@ -88,6 +86,7 @@ def tile_mspagent_pb_kernel(tc, h, gate_logit, e_w1, e_b1, e_w2, e_b2, out_0, ou
         load_w2(0)
         load_w1(2, 0)
         load_w1(2, 1)
+        nc.sync.dma_start(out=b2bc[:], in_=e_b2.rearrange("x a -> (x a)").partition_broadcast(P))
         load_w2(1)
         load_w1(3, 0)
         load_w1(3, 1)
@@ -182,24 +181,25 @@ def tile_mspagent_pb_kernel(tc, h, gate_logit, e_w1, e_b1, e_w2, e_b2, out_0, ou
         out1_view = out_1.rearrange("(p mt) x a -> p mt x a", mt=MT)
         out0_view = out_0.rearrange("(p mt) a -> p mt a", mt=MT)
 
-        def mm1(n, ts=(0, 1, 2, 3)):
+        def mm1(n, ts=(0, 1, 2, 3), lo=0, hi=512):
             ex, half = n // 2, n % 2
             if n not in s1_banks:
                 s1_banks[n] = {}
                 pl_tile = work.tile([P, 4, 512], BF16, name="planes", tag="planes")
                 planes[n] = pl_tile
             for t in ts:
-                bank = ps_s1.tile([P, 512], F32, name="s1_bank", tag="s1")
+                if lo == 0:
+                    bank = ps_s1.tile([P, 512], F32, name="s1_bank", tag="s1")
+                    s1_banks[n][t] = bank
                 nc.tensor.matmul_mx(
-                    out=bank[:],
+                    out=s1_banks[n][t][:, lo:hi],
                     lhsT=cod[("w1", ex)][:, t * P:(t + 1) * P].bitcast(FP8X4),
                     lhsT_scale=sca[("w1", ex)][:, t * P:(t + 1) * P],
-                    rhs=cod[("h", half)][:].bitcast(FP8X4),
-                    rhs_scale=sca[("h", half)][:],
+                    rhs=cod[("h", half)][:, lo:hi].bitcast(FP8X4),
+                    rhs_scale=sca[("h", half)][:, lo:hi],
                     start=True,
                     stop=True,
                 )
-                s1_banks[n][t] = bank
 
         def c1(n, t, lo=0, hi=512):
             ex = n // 2
@@ -288,9 +288,6 @@ def tile_mspagent_pb_kernel(tc, h, gate_logit, e_w1, e_b1, e_w2, e_b2, out_0, ou
                 nc.tensor.matmul(out=warm_bank[:], lhsT=ones[:, 0:P], rhs=ones[:], start=True, stop=True)
 
         warm_up(5)
-        job_t("h", 0, 0)
-        job_t("h", 0, 1)
-        warm_up(1)
         b1_bank = ps_s2.tile([P, 512], F32, name="b1_bank", tag="s2")
         b1T = keep.tile([P, 4 * NEXP], F32, name="b1T")
         for u in range(2):
@@ -300,38 +297,36 @@ def tile_mspagent_pb_kernel(tc, h, gate_logit, e_w1, e_b1, e_w2, e_b2, out_0, ou
                 out=b1T[:].rearrange("p (x u e) -> p x u e", u=2, e=2)[:, :, u, :],
                 in_=b1_bank[:, u * P:(u + 1) * P].bitcast(BF16)[:, 0:2 * NEXP].rearrange("p (x e) -> p x e", e=2),
             )
-
+        job_t("h", 0, 0)
         job_t("w1", 0, 0, "s1")
+        job_t("h", 0, 1)
         job_t("w1", 0, 1, "s1")
         job_x("h", 0, 0, "v")
-        job_x("h", 0, 1, "s")
-        job_q("h", 0, 0, 256)
         job_x("w1", 0, 0, "s")
-        b2bc = keep.tile([P, NEXP * NACT], F32, name="b2bc")
-        for c in range(2):
-            b2_bank = ps_s2.tile([P, 512], F32, name="b2_bank", tag="s2")
-            nc.tensor.matmul(out=b2_bank[:], lhsT=ones[:, 0:P], rhs=b2_row[:, c * 512:(c + 1) * 512], start=True, stop=True)
-            nc.scalar.copy(out=b2bc[:, c * 512:(c + 1) * 512], in_=b2_bank[:])
-        job_q("h", 0, 256, 512)
+        job_q("h", 0, 0, 256)
+        job_x("h", 0, 1, "s")
         job_q("w1", 0, 0, 256)
         job_x("w1", 0, 1, "v")
-        job_t("h", 1, 0)
-        job_x("h", 1, 0, "v")
+        job_q("h", 0, 256, 512)
         job_q("w1", 0, 256, 512)
-
-        mm1(0, (0, 1))
+        mm1(0, (0, 1), 0, 256)
+        job_t("h", 1, 0)
+        for t in range(2):
+            c1(0, t, 0, 256)
+        mm1(0, (0, 1), 256, 512)
         job_t("h", 1, 1)
         mm1(0, (2, 3))
-        job_x("h", 1, 1, "v")
-        for t in range(4):
+        for t in range(2):
+            c1(0, t, 256, 512)
+        for t in range(2, 4):
             c1(0, t)
+        job_x("h", 1, 0, "v")
+        job_x("h", 1, 1, "v")
         job_t("w1", 1, 0)
         job_t("w1", 1, 1)
-        job_x("w1", 1, 0, "v")
+        job_x("w1", 1, 0, "s")
         job_q("h", 1)
         job_x("w1", 1, 1, "v")
-        job_t("w2", 0, 0)
-        job_x("w2", 0, 0, "s")
 
         prep_plan = {
             0: ("w1", 2, "ss"),
@@ -358,6 +353,9 @@ def tile_mspagent_pb_kernel(tc, h, gate_logit, e_w1, e_b1, e_w2, e_b2, out_0, ou
                 for lo in (0, 256):
                     for t in range(4):
                         c1(LAST, t, lo, lo + 256)
+            if k == 0:
+                job_t("w2", 0, 0)
+                job_x("w2", 0, 0, "s")
             regroup(k, "s", 512 - S_COLS[k], 512)
             job = prep_plan.get(k)
             if job:

@@ -22,9 +22,6 @@ UNITS = NEXP * 2
 
 FLOPS = 2 * ROWS * H * H * NEXP + 2 * ROWS * H * NACT * NEXP
 
-S_COLS = [0] * 9 + [64] * 4 + [96, 128]
-S_LAST = 256
-
 
 def tile_mspagent_pb_kernel(tc, h, gate_logit, e_w1, e_b1, e_w2, e_b2, out_0, out_1):
     nc = tc.nc
@@ -38,15 +35,14 @@ def tile_mspagent_pb_kernel(tc, h, gate_logit, e_w1, e_b1, e_w2, e_b2, out_0, ou
 
         ident = keep.tile([P, P], F32, name="ident")
         make_identity(nc, ident[:])
-        ones = keep.tile([P, 512], BF16, name="ones")
-        nc.vector.memset(ones[:], 1.0)
         b1_rows = keep.tile([P, H], BF16, name="b1_rows")
         nc.vector.memset(b1_rows[:].bitcast(F32), 0.0)
+        ones = keep.tile([P, 512], BF16, name="ones")
+        nc.vector.memset(ones[:], 1.0)
         b2bc = keep.tile([P, NEXP * NACT], BF16, name="b2bc")
         gate = keep.tile([P, MT * NEXP], F32, name="gate")
 
         gl = keep.tile([P, MT * NEXP], BF16, name="gl")
-        nc.sync.dma_start(out=b1_rows[0:NEXP, :], in_=e_b1)
         nc.sync.dma_start(out=gl[:], in_=gate_logit.rearrange("(p mt) x -> p (mt x)", mt=MT))
 
         h_view = h.rearrange("(p mt) k -> p mt k", mt=MT)
@@ -76,6 +72,7 @@ def tile_mspagent_pb_kernel(tc, h, gate_logit, e_w1, e_b1, e_w2, e_b2, out_0, ou
             nc.sync.dma_start(out=w2_sb[q][:], in_=e_w2[2 * q:2 * q + 2].rearrange("x a k -> a x k"))
 
         load_h(0)
+        nc.sync.dma_start(out=b1_rows[0:NEXP, :], in_=e_b1)
         load_w1(0, 0)
         load_h(1)
         load_w1(0, 1)
@@ -209,8 +206,6 @@ def tile_mspagent_pb_kernel(tc, h, gate_logit, e_w1, e_b1, e_w2, e_b2, out_0, ou
             )
 
         def regroup(n, engine, lo, hi):
-            if lo == hi:
-                return
             if n not in h1_g:
                 g_tile = work.tile([P, 512 * 4], BF16, name="h1_g", tag="h1_g", align_bytes=64)
                 h1_g[n] = g_tile
@@ -288,6 +283,14 @@ def tile_mspagent_pb_kernel(tc, h, gate_logit, e_w1, e_b1, e_w2, e_b2, out_0, ou
                 nc.tensor.matmul(out=warm_bank[:], lhsT=ones[:, 0:P], rhs=ones[:], start=True, stop=True)
 
         warm_up(5)
+        job_t("h", 0, 0)
+        job_t("w1", 0, 0, "s1")
+        job_t("h", 0, 1)
+        job_t("w1", 0, 1, "s1")
+        job_x("h", 0, 0, "v")
+        job_x("w1", 0, 0, "s")
+        job_q("h", 0, 0, 256)
+        job_x("h", 0, 1, "s")
         b1_bank = ps_s2.tile([P, 512], F32, name="b1_bank", tag="s2")
         b1T = keep.tile([P, 4 * NEXP], F32, name="b1T")
         for u in range(2):
@@ -297,14 +300,6 @@ def tile_mspagent_pb_kernel(tc, h, gate_logit, e_w1, e_b1, e_w2, e_b2, out_0, ou
                 out=b1T[:].rearrange("p (x u e) -> p x u e", u=2, e=2)[:, :, u, :],
                 in_=b1_bank[:, u * P:(u + 1) * P].bitcast(BF16)[:, 0:2 * NEXP].rearrange("p (x e) -> p x e", e=2),
             )
-        job_t("h", 0, 0)
-        job_t("w1", 0, 0, "s1")
-        job_t("h", 0, 1)
-        job_t("w1", 0, 1, "s1")
-        job_x("h", 0, 0, "v")
-        job_x("w1", 0, 0, "s")
-        job_q("h", 0, 0, 256)
-        job_x("h", 0, 1, "s")
         job_q("w1", 0, 0, 256)
         job_x("w1", 0, 1, "v")
         job_q("h", 0, 256, 512)
@@ -355,17 +350,17 @@ def tile_mspagent_pb_kernel(tc, h, gate_logit, e_w1, e_b1, e_w2, e_b2, out_0, ou
                         c1(LAST, t, lo, lo + 256)
             if k == 0:
                 job_t("w2", 0, 0)
-                job_x("w2", 0, 0, "s")
-            regroup(k, "s", 512 - S_COLS[k], 512)
             job = prep_plan.get(k)
             if job:
                 for b in range(len(job[2])):
                     job_t(job[0], job[1], b)
                 for b in range(len(job[2])):
-                    job_x(job[0], job[1], b, job[2][b])
-            regroup(k, "v", 0, 512 - S_COLS[k])
+                    if job[2][b] == "s":
+                        job_x(job[0], job[1], b, "s")
+            regroup(k, "v", 0, 512)
             if k == 0:
                 job_q("w1", 1)
+                job_x("w2", 0, 0, "v")
             job = prep_plan.get(k - 1)
             if job:
                 job_q(job[0], job[1])
@@ -377,15 +372,18 @@ def tile_mspagent_pb_kernel(tc, h, gate_logit, e_w1, e_b1, e_w2, e_b2, out_0, ou
                 store(k - 1)
             else:
                 job_q("w2", 0)
+            job = prep_plan.get(k)
+            if job:
+                for b in range(len(job[2])):
+                    if job[2][b] == "v":
+                        job_x(job[0], job[1], b, "v")
 
         mm2(LAST - 1)
-        regroup(LAST, "s", 256 - S_LAST, 256)
-        regroup(LAST, "s", 512 - S_LAST, 512)
-        regroup(LAST, "v", 0, 256 - S_LAST)
+        regroup(LAST, "s", 0, 256)
+        regroup(LAST, "s", 256, 512)
         add_b2(LAST - 1)
         q1(LAST, 0, 256)
         mm2(LAST, (0, 1))
-        regroup(LAST, "v", 256, 512 - S_LAST)
         gate_sum(LAST - 1, 0, 2)
         q1(LAST, 256, 512)
         mm2(LAST, (2, 3))

@@ -20,6 +20,10 @@ MT = ROWS // P
 HALF_MT = 4
 UNITS = NEXP * 2
 
+PE_EXPERTS = (3, 4)
+Z_STEPS = {10: (6,), 11: (7,), 12: (8,), 13: (9,)}
+P_STEPS = {11: (6,), 12: (7,), 13: (8,), 14: (9,)}
+
 FLOPS = 2 * ROWS * H * H * NEXP + 2 * ROWS * H * NACT * NEXP
 
 
@@ -39,7 +43,9 @@ def tile_mspagent_pb_kernel(tc, h, gate_logit, e_w1, e_b1, e_w2, e_b2, out_0, ou
         nc.vector.memset(b1_rows[:].bitcast(F32), 0.0)
         ones = keep.tile([P, 512], BF16, name="ones")
         nc.vector.memset(ones[:], 1.0)
-        b2bc = keep.tile([P, NEXP * NACT], BF16, name="b2bc")
+        b2_row = keep.tile([P, NEXP * NACT], BF16, name="b2_row")
+        nc.vector.memset(b2_row[:].bitcast(F32), 0.0)
+        b2bc = keep.tile([P, NEXP * NACT], F32, name="b2bc")
         gate = keep.tile([P, MT * NEXP], F32, name="gate")
 
         gl = keep.tile([P, MT * NEXP], BF16, name="gl")
@@ -76,6 +82,7 @@ def tile_mspagent_pb_kernel(tc, h, gate_logit, e_w1, e_b1, e_w2, e_b2, out_0, ou
         load_w1(0, 0)
         load_h(1)
         load_w1(0, 1)
+        nc.sync.dma_start(out=b2_row[0:1, :], in_=e_b2.rearrange("(o x) a -> o (x a)", o=1))
         load_h(2)
         load_h(3)
         load_w1(1, 0)
@@ -83,7 +90,6 @@ def tile_mspagent_pb_kernel(tc, h, gate_logit, e_w1, e_b1, e_w2, e_b2, out_0, ou
         load_w2(0)
         load_w1(2, 0)
         load_w1(2, 1)
-        nc.sync.dma_start(out=b2bc[:], in_=e_b2.rearrange("x a -> (x a)").partition_broadcast(P))
         load_w2(1)
         load_w1(3, 0)
         load_w1(3, 1)
@@ -171,6 +177,8 @@ def tile_mspagent_pb_kernel(tc, h, gate_logit, e_w1, e_b1, e_w2, e_b2, out_0, ou
         h1_s = {}
         s2_bank = {}
         y_sb = {}
+        z_sb = {}
+        sum_bank = {}
         acc = []
         for half in range(2):
             acc_tile = keep.tile([P, HALF_MT, NACT], F32, name="acc%d" % half)
@@ -206,6 +214,8 @@ def tile_mspagent_pb_kernel(tc, h, gate_logit, e_w1, e_b1, e_w2, e_b2, out_0, ou
             )
 
         def regroup(n, engine, lo, hi):
+            if lo == hi:
+                return
             if n not in h1_g:
                 g_tile = work.tile([P, 512 * 4], BF16, name="h1_g", tag="h1_g", align_bytes=64)
                 h1_g[n] = g_tile
@@ -243,7 +253,7 @@ def tile_mspagent_pb_kernel(tc, h, gate_logit, e_w1, e_b1, e_w2, e_b2, out_0, ou
         def add_b2(n, lo=0, hi=HALF_MT):
             ex = n // 2
             if n not in y_sb:
-                y_tile = work.tile([P, HALF_MT, NACT], F32, name="y_sb", tag="y_sb", bufs=4)
+                y_tile = work.tile([P, HALF_MT, NACT], F32, name="y_sb", tag="y_sb", bufs=10)
                 y_sb[n] = y_tile
             nc.vector.tensor_tensor(
                 out=y_sb[n][:, lo:hi, :],
@@ -254,6 +264,8 @@ def tile_mspagent_pb_kernel(tc, h, gate_logit, e_w1, e_b1, e_w2, e_b2, out_0, ou
 
         def gate_sum(n, lo=0, hi=HALF_MT):
             ex, half = n // 2, n % 2
+            if ex in PE_EXPERTS:
+                return
             for i in range(lo, hi):
                 col = (half * HALF_MT + i) * NEXP + ex
                 if ex == 0:
@@ -265,10 +277,29 @@ def tile_mspagent_pb_kernel(tc, h, gate_logit, e_w1, e_b1, e_w2, e_b2, out_0, ou
                         out=acc[half][:, i, :],
                         in0=y_sb[n][:, i, :],
                         scalar=gate[:, col:col + 1],
-                        in1=acc[half][:, i, :],
+                        in1=sum_bank[half][:, i, :] if ex == NEXP - 1 else acc[half][:, i, :],
                         op0=ALU.mult,
                         op1=ALU.add,
                     )
+
+        def scale_by_gate(n):
+            z_tile = work.tile([P, HALF_MT, NACT], F32, name="z_sb", tag="z_sb", bufs=4)
+            z_sb[n] = z_tile
+            for i in range(HALF_MT):
+                col = ((n % 2) * HALF_MT + i) * NEXP + n // 2
+                nc.scalar.activation(out=z_tile[:, i, :], in_=y_sb[n][:, i, :], func=ACT.Copy, scale=gate[:, col:col + 1])
+
+        def bank_add(half, term, start, stop):
+            if start:
+                bank = ps_tp.tile([P, HALF_MT, NACT], F32, name="sum_bank", tag="tp")
+                sum_bank[half] = bank
+            nc.tensor.matmul(
+                out=sum_bank[half][:].rearrange("p i a -> p (i a)"),
+                lhsT=ident[:],
+                rhs=term[:].rearrange("p i a -> p (i a)"),
+                start=start,
+                stop=stop,
+            )
 
         def store(n, lo=0, hi=HALF_MT):
             ex, half = n // 2, n % 2
@@ -282,6 +313,16 @@ def tile_mspagent_pb_kernel(tc, h, gate_logit, e_w1, e_b1, e_w2, e_b2, out_0, ou
             for i in range(count):
                 nc.tensor.matmul(out=warm_bank[:], lhsT=ones[:, 0:P], rhs=ones[:], start=True, stop=True)
 
+        def spread_b2(c):
+            b2_bank = ps_s2.tile([P, 512], F32, name="b2_bank", tag="s2")
+            cols = slice(c * 512, (c + 1) * 512)
+            nc.tensor.matmul(out=b2_bank[:], lhsT=ones[:, 0:P], rhs=b2_row[:, cols], start=True, stop=True)
+            b2_banks[c] = b2_bank
+
+        def exit_b2(c):
+            nc.scalar.copy(out=b2bc[:, c * 512:(c + 1) * 512], in_=b2_banks[c][:])
+
+        b2_banks = {}
         warm_up(5)
         job_t("h", 0, 0)
         job_t("w1", 0, 0, "s1")
@@ -300,6 +341,7 @@ def tile_mspagent_pb_kernel(tc, h, gate_logit, e_w1, e_b1, e_w2, e_b2, out_0, ou
                 out=b1T[:].rearrange("p (x u e) -> p x u e", u=2, e=2)[:, :, u, :],
                 in_=b1_bank[:, u * P:(u + 1) * P].bitcast(BF16)[:, 0:2 * NEXP].rearrange("p (x e) -> p x e", e=2),
             )
+        spread_b2(0)
         job_q("w1", 0, 0, 256)
         job_x("w1", 0, 1, "v")
         job_q("h", 0, 256, 512)
@@ -308,6 +350,7 @@ def tile_mspagent_pb_kernel(tc, h, gate_logit, e_w1, e_b1, e_w2, e_b2, out_0, ou
         job_t("h", 1, 0)
         for t in range(2):
             c1(0, t, 0, 256)
+        exit_b2(0)
         mm1(0, (0, 1), 256, 512)
         job_t("h", 1, 1)
         mm1(0, (2, 3))
@@ -341,6 +384,10 @@ def tile_mspagent_pb_kernel(tc, h, gate_logit, e_w1, e_b1, e_w2, e_b2, out_0, ou
             mm1(k + 1)
             if k >= 1:
                 mm2(k - 1)
+            for n in P_STEPS.get(k, ()):
+                bank_add(n % 2, z_sb[n], n // 2 == PE_EXPERTS[0], False)
+            if k == 14:
+                bank_add(0, acc[0], False, True)
             if k + 1 < LAST:
                 for t in range(4):
                     c1(k + 1, t)
@@ -357,6 +404,11 @@ def tile_mspagent_pb_kernel(tc, h, gate_logit, e_w1, e_b1, e_w2, e_b2, out_0, ou
                 for b in range(len(job[2])):
                     if job[2][b] == "s":
                         job_x(job[0], job[1], b, "s")
+            if k == 3:
+                spread_b2(1)
+                exit_b2(1)
+            for n in Z_STEPS.get(k, ()):
+                scale_by_gate(n)
             regroup(k, "v", 0, 512)
             if k == 0:
                 job_q("w1", 1)
@@ -379,11 +431,14 @@ def tile_mspagent_pb_kernel(tc, h, gate_logit, e_w1, e_b1, e_w2, e_b2, out_0, ou
                         job_x(job[0], job[1], b, "v")
 
         mm2(LAST - 1)
-        regroup(LAST, "s", 0, 256)
-        regroup(LAST, "s", 256, 512)
+        bank_add(1, acc[1], False, True)
+        regroup(LAST, "s", 256 - 128, 256)
+        regroup(LAST, "s", 512 - 128, 512)
+        regroup(LAST, "v", 0, 256 - 128)
         add_b2(LAST - 1)
         q1(LAST, 0, 256)
         mm2(LAST, (0, 1))
+        regroup(LAST, "v", 256, 512 - 128)
         gate_sum(LAST - 1, 0, 2)
         q1(LAST, 256, 512)
         mm2(LAST, (2, 3))

@@ -326,6 +326,7 @@ def tile_mspagent_pb_kernel(tc, h, gate_logit, e_w1, e_b1, e_w2, e_b2, out_0, ou
         warm_up(5)
         job_t("h", 0, 0)
         job_t("w1", 0, 0, "s1")
+        warm_up(2)
         job_t("h", 0, 1)
         job_t("w1", 0, 1, "s1")
         job_x("h", 0, 0, "v")
@@ -341,6 +342,7 @@ def tile_mspagent_pb_kernel(tc, h, gate_logit, e_w1, e_b1, e_w2, e_b2, out_0, ou
                 out=b1T[:].rearrange("p (x u e) -> p x u e", u=2, e=2)[:, :, u, :],
                 in_=b1_bank[:, u * P:(u + 1) * P].bitcast(BF16)[:, 0:2 * NEXP].rearrange("p (x e) -> p x e", e=2),
             )
+        warm_up(1)
         spread_b2(0)
         job_q("w1", 0, 0, 256)
         job_x("w1", 0, 1, "v")
@@ -351,8 +353,8 @@ def tile_mspagent_pb_kernel(tc, h, gate_logit, e_w1, e_b1, e_w2, e_b2, out_0, ou
         for t in range(2):
             c1(0, t, 0, 256)
         exit_b2(0)
-        mm1(0, (0, 1), 256, 512)
         job_t("h", 1, 1)
+        mm1(0, (0, 1), 256, 512)
         mm1(0, (2, 3))
         for t in range(2):
             c1(0, t, 256, 512)
@@ -362,9 +364,9 @@ def tile_mspagent_pb_kernel(tc, h, gate_logit, e_w1, e_b1, e_w2, e_b2, out_0, ou
         job_x("h", 1, 1, "v")
         job_t("w1", 1, 0)
         job_t("w1", 1, 1)
-        job_x("w1", 1, 0, "s")
         job_q("h", 1)
-        job_x("w1", 1, 1, "v")
+        job_x("w1", 1, 0, "v")
+        job_x("w1", 1, 1, "s")
 
         prep_plan = {
             0: ("w1", 2, "ss"),

@@ -39,17 +39,16 @@ def tile_mspagent_pb_kernel(tc, h, gate_logit, e_w1, e_b1, e_w2, e_b2, out_0, ou
 
         ident = keep.tile([P, P], F32, name="ident")
         make_identity(nc, ident[:])
-        b1_rows = keep.tile([P, H], BF16, name="b1_rows")
-        nc.vector.memset(b1_rows[:].bitcast(F32), 0.0)
         ones = keep.tile([P, 512], BF16, name="ones")
         nc.vector.memset(ones[:], 1.0)
+        b1_rows = keep.tile([P, H], BF16, name="b1_rows")
+        nc.vector.memset(b1_rows[:].bitcast(F32), 0.0)
         b2_row = keep.tile([P, NEXP * NACT], BF16, name="b2_row")
         nc.vector.memset(b2_row[:].bitcast(F32), 0.0)
         b2bc = keep.tile([P, NEXP * NACT], F32, name="b2bc")
         gate = keep.tile([P, MT * NEXP], F32, name="gate")
 
         gl = keep.tile([P, MT * NEXP], BF16, name="gl")
-        nc.sync.dma_start(out=gl[:], in_=gate_logit.rearrange("(p mt) x -> p (mt x)", mt=MT))
 
         h_view = h.rearrange("(p mt) k -> p mt k", mt=MT)
         h_sb = []
@@ -77,11 +76,13 @@ def tile_mspagent_pb_kernel(tc, h, gate_logit, e_w1, e_b1, e_w2, e_b2, out_0, ou
         def load_w2(q):
             nc.sync.dma_start(out=w2_sb[q][:], in_=e_w2[2 * q:2 * q + 2].rearrange("x a k -> a x k"))
 
-        load_h(0)
-        nc.sync.dma_start(out=b1_rows[0:NEXP, :], in_=e_b1)
+        for s in range(2):
+            nc.sync.dma_start(out=h_sb[0][:, s, :], in_=h_view[:, s, :])
+        nc.sync.dma_start(out=gl[:], in_=gate_logit.rearrange("(p mt) x -> p (mt x)", mt=MT))
         load_w1(0, 0)
         load_h(1)
         load_w1(0, 1)
+        nc.sync.dma_start(out=b1_rows[0:NEXP, :], in_=e_b1)
         nc.sync.dma_start(out=b2_row[0:1, :], in_=e_b2.rearrange("(o x) a -> o (x a)", o=1))
         load_h(2)
         load_h(3)
@@ -323,7 +324,7 @@ def tile_mspagent_pb_kernel(tc, h, gate_logit, e_w1, e_b1, e_w2, e_b2, out_0, ou
             nc.scalar.copy(out=b2bc[:, c * 512:(c + 1) * 512], in_=b2_banks[c][:])
 
         b2_banks = {}
-        warm_up(5)
+        warm_up(4)
         job_t("h", 0, 0)
         job_t("w1", 0, 0, "s1")
         warm_up(2)

@@ -30,426 +30,428 @@ FLOPS = 2 * ROWS * H * H * NEXP + 2 * ROWS * H * NACT * NEXP
 def tile_mspagent_pb_kernel(tc, h, gate_logit, e_w1, e_b1, e_w2, e_b2, out_0, out_1):
     nc = tc.nc
     with ExitStack() as ctx:
-        ctx.enter_context(tc.manual_schedule())
         keep = ctx.enter_context(tc.tile_pool(name="keep", bufs=1))
         work = ctx.enter_context(tc.tile_pool(name="work", bufs=3))
         ps_s1 = ctx.enter_context(tc.psum_pool(name="ps_s1", bufs=4))
         ps_tp = ctx.enter_context(tc.psum_pool(name="ps_tp", bufs=2))
         ps_s2 = ctx.enter_context(tc.psum_pool(name="ps_s2", bufs=2))
 
-        ident = keep.tile([P, P], F32, name="ident")
-        make_identity(nc, ident[:])
-        ones = keep.tile([P, 512], BF16, name="ones")
-        nc.vector.memset(ones[:], 1.0)
-        b1_rows = keep.tile([P, H], BF16, name="b1_rows")
-        nc.vector.memset(b1_rows[:].bitcast(F32), 0.0)
-        b2_row = keep.tile([P, NEXP * NACT], BF16, name="b2_row")
-        nc.vector.memset(b2_row[:].bitcast(F32), 0.0)
-        b2bc = keep.tile([P, NEXP * NACT], F32, name="b2bc")
-        gate = keep.tile([P, MT * NEXP], F32, name="gate")
+        with tc.manual_schedule():
+            ident = keep.tile([P, P], F32, name="ident")
+            make_identity(nc, ident[:])
+            ones = keep.tile([P, 512], BF16, name="ones")
+            nc.vector.memset(ones[:], 1.0)
+            b2_row = keep.tile([P, NEXP * NACT], BF16, name="b2_row")
+            nc.vector.memset(b2_row[:].bitcast(F32), 0.0)
+            b1_rows = keep.tile([P, H], BF16, name="b1_rows")
+            nc.vector.memset(b1_rows[:].bitcast(F32), 0.0)
+            b2bc = keep.tile([P, NEXP * NACT], F32, name="b2bc")
+            gate = keep.tile([P, MT * NEXP], F32, name="gate")
 
-        gl = keep.tile([P, MT * NEXP], BF16, name="gl")
+            gl = keep.tile([P, MT * NEXP], BF16, name="gl")
 
-        h_view = h.rearrange("(p mt) k -> p mt k", mt=MT)
-        h_sb = []
-        w1_sb = []
-        w2_sb = []
-        for q in range(4):
-            h_tile = keep.tile([P, 2, H], BF16, name="h_sb%d" % q)
-            h_sb.append(h_tile)
-        for ex in range(NEXP):
-            for u in range(2):
-                w1_tile = keep.tile([P, 2, H], BF16, name="w1_sb%d_%d" % (ex, u))
-                w1_sb.append(w1_tile)
-        for q in range(4):
-            w2_tile = keep.tile([P, 2, H], BF16, name="w2_sb%d" % q)
-            w2_sb.append(w2_tile)
-
-        def load_h(q):
-            nc.sync.dma_start(out=h_sb[q][:], in_=h_view[:, 2 * q:2 * q + 2, :])
-
-        def load_w1(ex, u):
-            nc.sync.dma_start(
-                out=w1_sb[2 * ex + u][:], in_=e_w1[ex].rearrange("(p t) k -> p t k", t=4)[:, 2 * u:2 * u + 2, :]
-            )
-
-        def load_w2(q):
-            nc.sync.dma_start(out=w2_sb[q][:], in_=e_w2[2 * q:2 * q + 2].rearrange("x a k -> a x k"))
-
-        for s in range(2):
-            nc.sync.dma_start(out=h_sb[0][:, s, :], in_=h_view[:, s, :])
-        nc.sync.dma_start(out=gl[:], in_=gate_logit.rearrange("(p mt) x -> p (mt x)", mt=MT))
-        load_w1(0, 0)
-        load_h(1)
-        load_w1(0, 1)
-        nc.sync.dma_start(out=b1_rows[0:NEXP, :], in_=e_b1)
-        nc.sync.dma_start(out=b2_row[0:1, :], in_=e_b2.rearrange("(o x) a -> o (x a)", o=1))
-        load_h(2)
-        load_h(3)
-        load_w1(1, 0)
-        load_w1(1, 1)
-        load_w2(0)
-        load_w1(2, 0)
-        load_w1(2, 1)
-        load_w2(1)
-        load_w1(3, 0)
-        load_w1(3, 1)
-        load_w2(2)
-        load_w1(4, 0)
-        load_w1(4, 1)
-        load_w2(3)
-        for ex in range(5, NEXP):
-            load_w1(ex, 0)
-            load_w1(ex, 1)
-
-        nc.scalar.activation(out=gate[:], in_=gl[:], func=ACT.Sigmoid)
-
-        def t_bank(src_tile, pool_tag):
-            if pool_tag == "s1":
-                bank = ps_s1.tile([P, 2, 2, P], F32, name="tp_bank1", tag="s1")
-            else:
-                bank = ps_tp.tile([P, 2, 2, P], F32, name="tp_bank", tag="tp")
-            for s in range(2):
-                words = src_tile[:, s, :].bitcast(F32)
+            h_view = h.rearrange("(p mt) k -> p mt k", mt=MT)
+            h_sb = []
+            w1_sb = []
+            w2_sb = []
+            for q in range(4):
+                h_tile = keep.tile([P, 2, H], BF16, name="h_sb%d" % q)
+                h_sb.append(h_tile)
+            for ex in range(NEXP):
                 for u in range(2):
-                    nc.tensor.transpose(bank[:, s, u, :], words[:, u:2 * P:2], ident[:])
-            return bank
+                    w1_tile = keep.tile([P, 2, H], BF16, name="w1_sb%d_%d" % (ex, u))
+                    w1_sb.append(w1_tile)
+            for q in range(4):
+                w2_tile = keep.tile([P, 2, H], BF16, name="w2_sb%d" % q)
+                w2_sb.append(w2_tile)
 
-        def x_bank(bank, grouped, engine):
-            dst = grouped.bitcast(F32).rearrange("p (s c u) -> p s c u", s=2, u=2)
-            src = bank[:].rearrange("p s u c -> p s c u")
-            if engine == "v":
-                nc.vector.tensor_copy(out=dst, in_=src)
-            else:
-                nc.scalar.copy(out=dst, in_=src)
+            def load_h(q):
+                nc.sync.dma_start(out=h_sb[q][:], in_=h_view[:, 2 * q:2 * q + 2, :])
 
-        def quantise(grouped, codes, scales):
-            nc.vector.quantize_mx(out=codes.bitcast(FP8X4), scales=scales, in_=grouped)
-
-        grp = {}
-        cod = {}
-        sca = {}
-        for half in range(2):
-            g_tile = keep.tile([P, 512 * 4], BF16, name="h_g%d" % half, align_bytes=64)
-            c_tile = keep.tile([P, 512], U32, name="h_c%d" % half, align_bytes=64)
-            s_tile = keep.tile([P, 512], U8, name="h_s%d" % half, align_bytes=64)
-            grp[("h", half)] = g_tile
-            cod[("h", half)] = c_tile
-            sca[("h", half)] = s_tile
-        for ex in range(NEXP):
-            c_tile = keep.tile([P, 512], U32, name="w1_c%d" % ex, align_bytes=64)
-            s_tile = keep.tile([P, 512], U8, name="w1_s%d" % ex, align_bytes=64)
-            cod[("w1", ex)] = c_tile
-            sca[("w1", ex)] = s_tile
-        for q in range(4):
-            c_tile = keep.tile([P, 256], U32, name="w2_c%d" % q, align_bytes=64)
-            s_tile = keep.tile([P, 256], U8, name="w2_s%d" % q, align_bytes=64)
-            cod[("w2", q)] = c_tile
-            sca[("w2", q)] = s_tile
-        live_banks = {}
-
-        def job_t(kind, idx, b, pool_tag="tp"):
-            if kind == "w1" and b == 0:
-                g_tile = work.tile([P, 512 * 4], BF16, name="w1_g", tag="w1_g", align_bytes=64)
-                grp[(kind, idx)] = g_tile
-            if kind == "w2":
-                g_tile = work.tile([P, 256 * 4], BF16, name="w2_g", tag="w2_g", bufs=2, align_bytes=64)
-                grp[(kind, idx)] = g_tile
-            if kind == "h":
-                src_tile = h_sb[2 * idx + b]
-            elif kind == "w1":
-                src_tile = w1_sb[2 * idx + b]
-            else:
-                src_tile = w2_sb[idx]
-            live_banks[(kind, idx, b)] = t_bank(src_tile, pool_tag)
-
-        def job_x(kind, idx, b, engine):
-            x_bank(live_banks[(kind, idx, b)], grp[(kind, idx)][:, b * 1024:(b + 1) * 1024], engine)
-
-        def job_q(kind, idx, lo=0, hi=None):
-            width = cod[(kind, idx)].shape[1]
-            top = width if hi is None else hi
-            quantise(grp[(kind, idx)][:, 4 * lo:4 * top], cod[(kind, idx)][:, lo:top], sca[(kind, idx)][:, lo:top])
-
-        s1_banks = {}
-        planes = {}
-        h1_g = {}
-        h1_c = {}
-        h1_s = {}
-        s2_bank = {}
-        y_sb = {}
-        z_sb = {}
-        sum_bank = {}
-        acc = []
-        for half in range(2):
-            acc_tile = keep.tile([P, HALF_MT, NACT], F32, name="acc%d" % half)
-            acc.append(acc_tile)
-        out1_view = out_1.rearrange("(p mt) x a -> p mt x a", mt=MT)
-        out0_view = out_0.rearrange("(p mt) a -> p mt a", mt=MT)
-
-        def mm1(n, ts=(0, 1, 2, 3), lo=0, hi=512):
-            ex, half = n // 2, n % 2
-            if n not in s1_banks:
-                s1_banks[n] = {}
-                pl_tile = work.tile([P, 4, 512], BF16, name="planes", tag="planes")
-                planes[n] = pl_tile
-            for t in ts:
-                if lo == 0:
-                    bank = ps_s1.tile([P, 512], F32, name="s1_bank", tag="s1")
-                    s1_banks[n][t] = bank
-                nc.tensor.matmul_mx(
-                    out=s1_banks[n][t][:, lo:hi],
-                    lhsT=cod[("w1", ex)][:, t * P:(t + 1) * P].bitcast(FP8X4),
-                    lhsT_scale=sca[("w1", ex)][:, t * P:(t + 1) * P],
-                    rhs=cod[("h", half)][:, lo:hi].bitcast(FP8X4),
-                    rhs_scale=sca[("h", half)][:, lo:hi],
-                    start=True,
-                    stop=True,
+            def load_w1(ex, u):
+                nc.sync.dma_start(
+                    out=w1_sb[2 * ex + u][:], in_=e_w1[ex].rearrange("(p t) k -> p t k", t=4)[:, 2 * u:2 * u + 2, :]
                 )
 
-        def c1(n, t, lo=0, hi=512):
-            ex = n // 2
-            bias = b1T[:, 4 * ex + t:4 * ex + t + 1]
-            nc.scalar.activation(
-                out=planes[n][:, t, lo:hi], in_=s1_banks[n][t][:, lo:hi], func=ACT.Relu, bias=bias, scale=1.0
-            )
+            def load_w2(q):
+                nc.sync.dma_start(out=w2_sb[q][:], in_=e_w2[2 * q:2 * q + 2].rearrange("x a k -> a x k"))
 
-        def regroup(n, engine, lo, hi):
-            if lo == hi:
-                return
-            if n not in h1_g:
-                g_tile = work.tile([P, 512 * 4], BF16, name="h1_g", tag="h1_g", align_bytes=64)
-                h1_g[n] = g_tile
-            dst = h1_g[n][:, 4 * lo:4 * hi].rearrange("p (c i t) -> p c t i", i=4, t=4)
-            src = planes[n][:, :, lo:hi].rearrange("p t (c i) -> p c t i", i=4)
-            if engine == "v":
-                nc.vector.tensor_copy(out=dst, in_=src)
-            else:
-                nc.scalar.copy(out=dst, in_=src)
+            for s in range(2):
+                nc.sync.dma_start(out=h_sb[0][:, s, :], in_=h_view[:, s, :])
+            nc.sync.dma_start(out=gl[:], in_=gate_logit.rearrange("(p mt) x -> p (mt x)", mt=MT))
+            load_w1(0, 0)
+            load_h(1)
+            load_w1(0, 1)
+            nc.sync.dma_start(out=b2_row[0:1, :], in_=e_b2.rearrange("(o x) a -> o (x a)", o=1))
+            nc.sync.dma_start(out=b1_rows[0:NEXP, :], in_=e_b1)
+            load_h(2)
+            load_h(3)
+            load_w1(1, 0)
+            load_w1(1, 1)
+            load_w2(0)
+            load_w1(2, 0)
+            load_w1(2, 1)
+            load_w2(1)
+            load_w1(3, 0)
+            load_w1(3, 1)
+            load_w2(2)
+            load_w1(4, 0)
+            load_w1(4, 1)
+            load_w2(3)
+            for ex in range(5, NEXP):
+                load_w1(ex, 0)
+                load_w1(ex, 1)
 
-        def q1(n, lo=0, hi=512):
-            if n not in h1_c:
-                c_tile = work.tile([P, 512], U32, name="h1_c", tag="h1_c", align_bytes=64)
-                s_tile = work.tile([P, 512], U8, name="h1_s", tag="h1_s", align_bytes=64)
-                h1_c[n] = c_tile
-                h1_s[n] = s_tile
-            quantise(h1_g[n][:, 4 * lo:4 * hi], h1_c[n][:, lo:hi], h1_s[n][:, lo:hi])
+            nc.scalar.activation(out=gate[:], in_=gl[:], func=ACT.Sigmoid)
 
-        def mm2(n, tiles=(0, 1, 2, 3)):
-            ex = n // 2
-            bank = ps_s2.tile([P, HALF_MT, NACT], F32, name="s2_bank", tag="s2")
-            lo = (ex % 2) * NACT
-            for i in tiles:
-                s2_bank[(n, i)] = bank
-                nc.tensor.matmul_mx(
-                    out=bank[:, i, :],
-                    lhsT=h1_c[n][:, i * P:(i + 1) * P].bitcast(FP8X4),
-                    lhsT_scale=h1_s[n][:, i * P:(i + 1) * P],
-                    rhs=cod[("w2", ex // 2)][:, lo:lo + NACT].bitcast(FP8X4),
-                    rhs_scale=sca[("w2", ex // 2)][:, lo:lo + NACT],
-                    start=True,
-                    stop=True,
-                )
-
-        def add_b2(n, lo=0, hi=HALF_MT):
-            ex = n // 2
-            if n not in y_sb:
-                y_tile = work.tile([P, HALF_MT, NACT], F32, name="y_sb", tag="y_sb", bufs=10)
-                y_sb[n] = y_tile
-            nc.vector.tensor_tensor(
-                out=y_sb[n][:, lo:hi, :],
-                in0=s2_bank[(n, lo)][:, lo:hi, :],
-                in1=b2bc[:, ex * NACT:(ex + 1) * NACT].unsqueeze(1).to_broadcast([P, hi - lo, NACT]),
-                op=ALU.add,
-            )
-
-        def gate_sum(n, lo=0, hi=HALF_MT):
-            ex, half = n // 2, n % 2
-            if ex in PE_EXPERTS:
-                return
-            for i in range(lo, hi):
-                col = (half * HALF_MT + i) * NEXP + ex
-                if ex == 0:
-                    nc.vector.tensor_scalar(
-                        out=acc[half][:, i, :], in0=y_sb[n][:, i, :], scalar1=gate[:, col:col + 1], scalar2=None, op0=ALU.mult
-                    )
+            def t_bank(src_tile, pool_tag, dummies):
+                if pool_tag == "s1":
+                    bank = ps_s1.tile([P, 2, 2, P], F32, name="tp_bank1", tag="s1")
                 else:
-                    nc.vector.scalar_tensor_tensor(
-                        out=acc[half][:, i, :],
-                        in0=y_sb[n][:, i, :],
-                        scalar=gate[:, col:col + 1],
-                        in1=sum_bank[half][:, i, :] if ex == NEXP - 1 else acc[half][:, i, :],
-                        op0=ALU.mult,
-                        op1=ALU.add,
+                    bank = ps_tp.tile([P, 2, 2, P], F32, name="tp_bank", tag="tp")
+                for i in range(dummies):
+                    nc.tensor.matmul(
+                        out=bank[:].rearrange("p s u c -> p (s u c)"), lhsT=ones[:, 0:P], rhs=ones[:], start=True, stop=True
+                    )
+                for s in range(2):
+                    words = src_tile[:, s, :].bitcast(F32)
+                    for u in range(2):
+                        nc.tensor.transpose(bank[:, s, u, :], words[:, u:2 * P:2], ident[:])
+                return bank
+
+            def x_bank(bank, grouped, engine):
+                dst = grouped.bitcast(F32).rearrange("p (s c u) -> p s c u", s=2, u=2)
+                src = bank[:].rearrange("p s u c -> p s c u")
+                if engine == "v":
+                    nc.vector.tensor_copy(out=dst, in_=src)
+                else:
+                    nc.scalar.copy(out=dst, in_=src)
+
+            def quantise(grouped, codes, scales):
+                nc.vector.quantize_mx(out=codes.bitcast(FP8X4), scales=scales, in_=grouped)
+
+            grp = {}
+            cod = {}
+            sca = {}
+            for half in range(2):
+                g_tile = keep.tile([P, 512 * 4], BF16, name="h_g%d" % half, align_bytes=64)
+                c_tile = keep.tile([P, 512], U32, name="h_c%d" % half, align_bytes=64)
+                s_tile = keep.tile([P, 512], U8, name="h_s%d" % half, align_bytes=64)
+                grp[("h", half)] = g_tile
+                cod[("h", half)] = c_tile
+                sca[("h", half)] = s_tile
+            for ex in range(NEXP):
+                c_tile = keep.tile([P, 512], U32, name="w1_c%d" % ex, align_bytes=64)
+                s_tile = keep.tile([P, 512], U8, name="w1_s%d" % ex, align_bytes=64)
+                cod[("w1", ex)] = c_tile
+                sca[("w1", ex)] = s_tile
+            for q in range(4):
+                c_tile = keep.tile([P, 256], U32, name="w2_c%d" % q, align_bytes=64)
+                s_tile = keep.tile([P, 256], U8, name="w2_s%d" % q, align_bytes=64)
+                cod[("w2", q)] = c_tile
+                sca[("w2", q)] = s_tile
+            live_banks = {}
+
+            def job_t(kind, idx, b, pool_tag="tp", dummies=0):
+                if kind == "w1" and b == 0:
+                    g_tile = work.tile([P, 512 * 4], BF16, name="w1_g", tag="w1_g", align_bytes=64)
+                    grp[(kind, idx)] = g_tile
+                if kind == "w2":
+                    g_tile = work.tile([P, 256 * 4], BF16, name="w2_g", tag="w2_g", bufs=2, align_bytes=64)
+                    grp[(kind, idx)] = g_tile
+                if kind == "h":
+                    src_tile = h_sb[2 * idx + b]
+                elif kind == "w1":
+                    src_tile = w1_sb[2 * idx + b]
+                else:
+                    src_tile = w2_sb[idx]
+                live_banks[(kind, idx, b)] = t_bank(src_tile, pool_tag, dummies)
+
+            def job_x(kind, idx, b, engine):
+                x_bank(live_banks[(kind, idx, b)], grp[(kind, idx)][:, b * 1024:(b + 1) * 1024], engine)
+
+            def job_q(kind, idx, lo=0, hi=None):
+                width = cod[(kind, idx)].shape[1]
+                top = width if hi is None else hi
+                quantise(grp[(kind, idx)][:, 4 * lo:4 * top], cod[(kind, idx)][:, lo:top], sca[(kind, idx)][:, lo:top])
+
+            s1_banks = {}
+            planes = {}
+            h1_g = {}
+            h1_c = {}
+            h1_s = {}
+            s2_bank = {}
+            y_sb = {}
+            z_sb = {}
+            sum_bank = {}
+            acc = []
+            for half in range(2):
+                acc_tile = keep.tile([P, HALF_MT, NACT], F32, name="acc%d" % half)
+                acc.append(acc_tile)
+            out1_view = out_1.rearrange("(p mt) x a -> p mt x a", mt=MT)
+            out0_view = out_0.rearrange("(p mt) a -> p mt a", mt=MT)
+
+            def mm1(n, ts=(0, 1, 2, 3), lo=0, hi=512):
+                ex, half = n // 2, n % 2
+                if n not in s1_banks:
+                    s1_banks[n] = {}
+                    pl_tile = work.tile([P, 4, 512], BF16, name="planes", tag="planes")
+                    planes[n] = pl_tile
+                for t in ts:
+                    if lo == 0:
+                        bank = ps_s1.tile([P, 512], F32, name="s1_bank", tag="s1")
+                        s1_banks[n][t] = bank
+                    nc.tensor.matmul_mx(
+                        out=s1_banks[n][t][:, lo:hi],
+                        lhsT=cod[("w1", ex)][:, t * P:(t + 1) * P].bitcast(FP8X4),
+                        lhsT_scale=sca[("w1", ex)][:, t * P:(t + 1) * P],
+                        rhs=cod[("h", half)][:, lo:hi].bitcast(FP8X4),
+                        rhs_scale=sca[("h", half)][:, lo:hi],
+                        start=True,
+                        stop=True,
                     )
 
-        def scale_by_gate(n):
-            z_tile = work.tile([P, HALF_MT, NACT], F32, name="z_sb", tag="z_sb", bufs=4)
-            z_sb[n] = z_tile
-            for i in range(HALF_MT):
-                col = ((n % 2) * HALF_MT + i) * NEXP + n // 2
-                nc.scalar.activation(out=z_tile[:, i, :], in_=y_sb[n][:, i, :], func=ACT.Copy, scale=gate[:, col:col + 1])
+            def c1(n, t, lo=0, hi=512):
+                ex = n // 2
+                bias = b1T[:, 4 * ex + t:4 * ex + t + 1]
+                nc.scalar.activation(
+                    out=planes[n][:, t, lo:hi], in_=s1_banks[n][t][:, lo:hi], func=ACT.Relu, bias=bias, scale=1.0
+                )
 
-        def bank_add(half, term, start, stop):
-            if start:
-                bank = ps_tp.tile([P, HALF_MT, NACT], F32, name="sum_bank", tag="tp")
-                sum_bank[half] = bank
-            nc.tensor.matmul(
-                out=sum_bank[half][:].rearrange("p i a -> p (i a)"),
-                lhsT=ident[:],
-                rhs=term[:].rearrange("p i a -> p (i a)"),
-                start=start,
-                stop=stop,
-            )
+            def regroup(n, engine, lo, hi):
+                if lo == hi:
+                    return
+                if n not in h1_g:
+                    g_tile = work.tile([P, 512 * 4], BF16, name="h1_g", tag="h1_g", align_bytes=64)
+                    h1_g[n] = g_tile
+                dst = h1_g[n][:, 4 * lo:4 * hi].rearrange("p (c i t) -> p c t i", i=4, t=4)
+                src = planes[n][:, :, lo:hi].rearrange("p t (c i) -> p c t i", i=4)
+                if engine == "v":
+                    nc.vector.tensor_copy(out=dst, in_=src)
+                else:
+                    nc.scalar.copy(out=dst, in_=src)
 
-        def store(n, lo=0, hi=HALF_MT):
-            ex, half = n // 2, n % 2
-            a, b = half * HALF_MT + lo, half * HALF_MT + hi
-            nc.sync.dma_start(out=out1_view[:, a:b, ex, :], in_=y_sb[n][:, lo:hi, :])
-            if ex == NEXP - 1:
-                nc.sync.dma_start(out=out0_view[:, a:b, :], in_=acc[half][:, lo:hi, :])
+            def q1(n, lo=0, hi=512):
+                if n not in h1_c:
+                    c_tile = work.tile([P, 512], U32, name="h1_c", tag="h1_c", align_bytes=64)
+                    s_tile = work.tile([P, 512], U8, name="h1_s", tag="h1_s", align_bytes=64)
+                    h1_c[n] = c_tile
+                    h1_s[n] = s_tile
+                quantise(h1_g[n][:, 4 * lo:4 * hi], h1_c[n][:, lo:hi], h1_s[n][:, lo:hi])
 
-        def warm_up(count):
-            warm_bank = ps_s2.tile([P, 512], F32, name="warm_bank", tag="s2")
-            for i in range(count):
-                nc.tensor.matmul(out=warm_bank[:], lhsT=ones[:, 0:P], rhs=ones[:], start=True, stop=True)
+            def mm2(n, tiles=(0, 1, 2, 3)):
+                ex = n // 2
+                bank = ps_s2.tile([P, HALF_MT, NACT], F32, name="s2_bank", tag="s2")
+                lo = (ex % 2) * NACT
+                for i in tiles:
+                    s2_bank[(n, i)] = bank
+                    nc.tensor.matmul_mx(
+                        out=bank[:, i, :],
+                        lhsT=h1_c[n][:, i * P:(i + 1) * P].bitcast(FP8X4),
+                        lhsT_scale=h1_s[n][:, i * P:(i + 1) * P],
+                        rhs=cod[("w2", ex // 2)][:, lo:lo + NACT].bitcast(FP8X4),
+                        rhs_scale=sca[("w2", ex // 2)][:, lo:lo + NACT],
+                        start=True,
+                        stop=True,
+                    )
 
-        def spread_b2(c):
-            b2_bank = ps_s2.tile([P, 512], F32, name="b2_bank", tag="s2")
-            cols = slice(c * 512, (c + 1) * 512)
-            nc.tensor.matmul(out=b2_bank[:], lhsT=ones[:, 0:P], rhs=b2_row[:, cols], start=True, stop=True)
-            b2_banks[c] = b2_bank
+            def add_b2(n, lo=0, hi=HALF_MT):
+                ex = n // 2
+                if n not in y_sb:
+                    y_tile = work.tile([P, HALF_MT, NACT], F32, name="y_sb", tag="y_sb", bufs=10)
+                    y_sb[n] = y_tile
+                nc.vector.tensor_tensor(
+                    out=y_sb[n][:, lo:hi, :],
+                    in0=s2_bank[(n, lo)][:, lo:hi, :],
+                    in1=b2bc[:, ex * NACT:(ex + 1) * NACT].unsqueeze(1).to_broadcast([P, hi - lo, NACT]),
+                    op=ALU.add,
+                )
 
-        def exit_b2(c):
-            nc.scalar.copy(out=b2bc[:, c * 512:(c + 1) * 512], in_=b2_banks[c][:])
+            def gate_sum(n, lo=0, hi=HALF_MT):
+                ex, half = n // 2, n % 2
+                if ex in PE_EXPERTS:
+                    return
+                for i in range(lo, hi):
+                    col = (half * HALF_MT + i) * NEXP + ex
+                    if ex == 0:
+                        nc.vector.tensor_scalar(
+                            out=acc[half][:, i, :], in0=y_sb[n][:, i, :], scalar1=gate[:, col:col + 1], scalar2=None, op0=ALU.mult
+                        )
+                    else:
+                        nc.vector.scalar_tensor_tensor(
+                            out=acc[half][:, i, :],
+                            in0=y_sb[n][:, i, :],
+                            scalar=gate[:, col:col + 1],
+                            in1=sum_bank[half][:, i, :] if ex == NEXP - 1 else acc[half][:, i, :],
+                            op0=ALU.mult,
+                            op1=ALU.add,
+                        )
 
-        b2_banks = {}
-        warm_up(4)
-        job_t("h", 0, 0)
-        job_t("w1", 0, 0, "s1")
-        warm_up(2)
-        job_t("h", 0, 1)
-        job_t("w1", 0, 1, "s1")
-        job_x("h", 0, 0, "v")
-        job_x("w1", 0, 0, "s")
-        job_q("h", 0, 0, 256)
-        job_x("h", 0, 1, "s")
-        b1_bank = ps_s2.tile([P, 512], F32, name="b1_bank", tag="s2")
-        b1T = keep.tile([P, 4 * NEXP], F32, name="b1T")
-        for u in range(2):
-            nc.tensor.transpose(b1_bank[:, u * P:(u + 1) * P], b1_rows[:].bitcast(F32)[:, u:2 * P:2], ident[:])
-        for u in range(2):
-            nc.scalar.copy(
-                out=b1T[:].rearrange("p (x u e) -> p x u e", u=2, e=2)[:, :, u, :],
-                in_=b1_bank[:, u * P:(u + 1) * P].bitcast(BF16)[:, 0:2 * NEXP].rearrange("p (x e) -> p x e", e=2),
-            )
-        warm_up(1)
-        spread_b2(0)
-        job_q("w1", 0, 0, 256)
-        job_x("w1", 0, 1, "v")
-        job_q("h", 0, 256, 512)
-        job_q("w1", 0, 256, 512)
-        mm1(0, (0, 1), 0, 256)
-        job_t("h", 1, 0)
-        for t in range(2):
-            c1(0, t, 0, 256)
-        exit_b2(0)
-        job_t("h", 1, 1)
-        mm1(0, (0, 1), 256, 512)
-        mm1(0, (2, 3))
-        for t in range(2):
-            c1(0, t, 256, 512)
-        for t in range(2, 4):
-            c1(0, t)
-        job_x("h", 1, 0, "v")
-        job_x("h", 1, 1, "v")
-        job_t("w1", 1, 0)
-        job_t("w1", 1, 1)
-        job_q("h", 1)
-        job_x("w1", 1, 0, "v")
-        job_x("w1", 1, 1, "s")
+            def scale_by_gate(n):
+                z_tile = work.tile([P, HALF_MT, NACT], F32, name="z_sb", tag="z_sb", bufs=4)
+                z_sb[n] = z_tile
+                for i in range(HALF_MT):
+                    col = ((n % 2) * HALF_MT + i) * NEXP + n // 2
+                    nc.scalar.activation(out=z_tile[:, i, :], in_=y_sb[n][:, i, :], func=ACT.Copy, scale=gate[:, col:col + 1])
 
-        prep_plan = {
-            0: ("w1", 2, "ss"),
-            1: ("w2", 1, "s"),
-            2: ("w1", 3, "ss"),
-            3: ("w1", 4, "ss"),
-            5: ("w2", 2, "s"),
-            6: ("w1", 5, "ss"),
-            7: ("w1", 6, "ss"),
-            9: ("w2", 3, "s"),
-            10: ("w1", 7, "ss"),
-        }
+            def bank_add(half, term, start, stop):
+                if start:
+                    bank = ps_tp.tile([P, HALF_MT, NACT], F32, name="sum_bank", tag="tp")
+                    sum_bank[half] = bank
+                nc.tensor.matmul(
+                    out=sum_bank[half][:].rearrange("p i a -> p (i a)"),
+                    lhsT=ident[:],
+                    rhs=term[:].rearrange("p i a -> p (i a)"),
+                    start=start,
+                    stop=stop,
+                )
 
-        nc.vector.tensor_scalar(out=gate[:], in0=gate[:], scalar1=1.0 / NEXP, scalar2=None, op0=ALU.mult)
-        LAST = UNITS - 1
-        for k in range(LAST):
-            mm1(k + 1)
-            if k >= 1:
-                mm2(k - 1)
-            for n in P_STEPS.get(k, ()):
-                bank_add(n % 2, z_sb[n], n // 2 == PE_EXPERTS[0], False)
-            if k == 14:
-                bank_add(0, acc[0], False, True)
-            if k + 1 < LAST:
-                for t in range(4):
-                    c1(k + 1, t)
-            else:
-                for lo in (0, 256):
+            def store(n, lo=0, hi=HALF_MT):
+                ex, half = n // 2, n % 2
+                a, b = half * HALF_MT + lo, half * HALF_MT + hi
+                nc.sync.dma_start(out=out1_view[:, a:b, ex, :], in_=y_sb[n][:, lo:hi, :])
+                if ex == NEXP - 1:
+                    nc.sync.dma_start(out=out0_view[:, a:b, :], in_=acc[half][:, lo:hi, :])
+
+            def warm_up(count):
+                warm_bank = ps_s2.tile([P, 512], F32, name="warm_bank", tag="s2")
+                for i in range(count):
+                    nc.tensor.matmul(out=warm_bank[:], lhsT=ones[:, 0:P], rhs=ones[:], start=True, stop=True)
+
+            def spread_b2(c):
+                b2_bank = ps_s2.tile([P, 512], F32, name="b2_bank", tag="s2")
+                cols = slice(c * 512, (c + 1) * 512)
+                nc.tensor.matmul(out=b2_bank[:], lhsT=ones[:, 0:P], rhs=b2_row[:, cols], start=True, stop=True)
+                b2_banks[c] = b2_bank
+
+            def exit_b2(c):
+                nc.scalar.copy(out=b2bc[:, c * 512:(c + 1) * 512], in_=b2_banks[c][:])
+
+            b2_banks = {}
+            warm_up(4)
+            job_t("h", 0, 0)
+            job_t("w1", 0, 0, "s1")
+            for c in range(2):
+                spread_b2(c)
+            job_t("h", 0, 1)
+            job_t("w1", 0, 1, "s1")
+            job_x("h", 0, 0, "v")
+            job_x("w1", 0, 0, "s")
+            job_q("h", 0, 0, 256)
+            exit_b2(0)
+            job_x("h", 0, 1, "s")
+            b1_bank = ps_s2.tile([P, 512], F32, name="b1_bank", tag="s2")
+            b1T = keep.tile([P, 4 * NEXP], F32, name="b1T")
+            for u in range(2):
+                nc.tensor.transpose(b1_bank[:, u * P:(u + 1) * P], b1_rows[:].bitcast(F32)[:, u:2 * P:2], ident[:])
+            for u in range(2):
+                nc.scalar.copy(
+                    out=b1T[:].rearrange("p (x u e) -> p x u e", u=2, e=2)[:, :, u, :],
+                    in_=b1_bank[:, u * P:(u + 1) * P].bitcast(BF16)[:, 0:2 * NEXP].rearrange("p (x e) -> p x e", e=2),
+                )
+            job_q("w1", 0, 0, 256)
+            job_x("w1", 0, 1, "v")
+            job_q("h", 0, 256, 512)
+            job_q("w1", 0, 256, 512)
+            mm1(0, (0, 1), 0, 256)
+            job_t("h", 1, 0, dummies=1)
+            for t in range(2):
+                c1(0, t, 0, 256)
+            exit_b2(1)
+            job_t("h", 1, 1)
+            mm1(0, (0, 1), 256, 512)
+            mm1(0, (2, 3))
+            for t in range(2):
+                c1(0, t, 256, 512)
+            for t in range(2, 4):
+                c1(0, t)
+            job_x("h", 1, 0, "v")
+            job_x("h", 1, 1, "v")
+            job_t("w1", 1, 0)
+            job_t("w1", 1, 1)
+            job_q("h", 1)
+            job_x("w1", 1, 0, "v")
+            job_x("w1", 1, 1, "s")
+
+            prep_plan = {
+                0: ("w1", 2, "ss"),
+                1: ("w2", 1, "s"),
+                2: ("w1", 3, "ss"),
+                3: ("w1", 4, "ss"),
+                5: ("w2", 2, "s"),
+                6: ("w1", 5, "ss"),
+                7: ("w1", 6, "ss"),
+                9: ("w2", 3, "s"),
+                10: ("w1", 7, "ss"),
+            }
+
+            nc.vector.tensor_scalar(out=gate[:], in0=gate[:], scalar1=1.0 / NEXP, scalar2=None, op0=ALU.mult)
+        with tc.manual_schedule(engines={mybir.EngineType.DVE, mybir.EngineType.SP}):
+            LAST = UNITS - 1
+            for k in range(LAST):
+                mm1(k + 1)
+                if k >= 1:
+                    mm2(k - 1)
+                for n in P_STEPS.get(k, ()):
+                    bank_add(n % 2, z_sb[n], n // 2 == PE_EXPERTS[0], False)
+                if k == 14:
+                    bank_add(0, acc[0], False, True)
+                if k + 1 < LAST:
                     for t in range(4):
-                        c1(LAST, t, lo, lo + 256)
-            if k == 0:
-                job_t("w2", 0, 0)
-            job = prep_plan.get(k)
-            if job:
-                for b in range(len(job[2])):
-                    job_t(job[0], job[1], b)
-                for b in range(len(job[2])):
-                    if job[2][b] == "s":
-                        job_x(job[0], job[1], b, "s")
-            if k == 3:
-                spread_b2(1)
-                exit_b2(1)
-            for n in Z_STEPS.get(k, ()):
-                scale_by_gate(n)
-            regroup(k, "v", 0, 512)
-            if k == 0:
-                job_q("w1", 1)
-                job_x("w2", 0, 0, "v")
-            job = prep_plan.get(k - 1)
-            if job:
-                job_q(job[0], job[1])
-            if k >= 1:
-                add_b2(k - 1)
-            q1(k)
-            if k >= 1:
-                gate_sum(k - 1)
-                store(k - 1)
-            else:
-                job_q("w2", 0)
-            job = prep_plan.get(k)
-            if job:
-                for b in range(len(job[2])):
-                    if job[2][b] == "v":
-                        job_x(job[0], job[1], b, "v")
+                        c1(k + 1, t)
+                else:
+                    for lo in (0, 256):
+                        for t in range(4):
+                            c1(LAST, t, lo, lo + 256)
+                if k == 0:
+                    job_t("w2", 0, 0)
+                job = prep_plan.get(k)
+                if job:
+                    for b in range(len(job[2])):
+                        job_t(job[0], job[1], b)
+                    for b in range(len(job[2])):
+                        if job[2][b] == "s":
+                            job_x(job[0], job[1], b, "s")
+                for n in Z_STEPS.get(k, ()):
+                    scale_by_gate(n)
+                regroup(k, "v", 0, 512)
+                if k == 0:
+                    job_q("w1", 1)
+                    job_x("w2", 0, 0, "v")
+                job = prep_plan.get(k - 1)
+                if job:
+                    job_q(job[0], job[1])
+                if k >= 1:
+                    add_b2(k - 1)
+                q1(k)
+                if k >= 1:
+                    gate_sum(k - 1)
+                    store(k - 1)
+                else:
+                    job_q("w2", 0)
+                job = prep_plan.get(k)
+                if job:
+                    for b in range(len(job[2])):
+                        if job[2][b] == "v":
+                            job_x(job[0], job[1], b, "v")
 
-        mm2(LAST - 1)
-        bank_add(1, acc[1], False, True)
-        regroup(LAST, "s", 256 - 128, 256)
-        regroup(LAST, "s", 512 - 128, 512)
-        regroup(LAST, "v", 0, 256 - 128)
-        add_b2(LAST - 1)
-        q1(LAST, 0, 256)
-        mm2(LAST, (0, 1))
-        regroup(LAST, "v", 256, 512 - 128)
-        gate_sum(LAST - 1, 0, 2)
-        q1(LAST, 256, 512)
-        mm2(LAST, (2, 3))
-        gate_sum(LAST - 1, 2, 4)
-        store(LAST - 1)
-        add_b2(LAST, 0, 2)
-        add_b2(LAST, 2, 4)
-        gate_sum(LAST, 0, 2)
-        store(LAST, 0, 2)
-        gate_sum(LAST, 2, 4)
-        store(LAST, 2, 4)
+            mm2(LAST - 1)
+            bank_add(1, acc[1], False, True)
+            regroup(LAST, "s", 256 - 192, 256)
+            regroup(LAST, "s", 512 - 256, 512)
+            regroup(LAST, "v", 0, 256 - 192)
+            add_b2(LAST - 1)
+            q1(LAST, 0, 256)
+            mm2(LAST, (0, 1))
+            regroup(LAST, "v", 256, 512 - 256)
+            gate_sum(LAST - 1, 0, 2)
+            q1(LAST, 256, 512)
+            mm2(LAST, (2, 3))
+            gate_sum(LAST - 1, 2, 4)
+            store(LAST - 1)
+            add_b2(LAST, 0, 2)
+            add_b2(LAST, 2, 4)
+            gate_sum(LAST, 0, 2)
+            store(LAST, 0, 2)
+            gate_sum(LAST, 2, 4)
+            store(LAST, 2, 4)

from contextlib import ExitStack

import concourse.mybir as mybir
from concourse.masks import make_identity

F32 = mybir.dt.float32
BF16 = mybir.dt.bfloat16
U32 = mybir.dt.uint32
U8 = mybir.dt.uint8
FP8X4 = mybir.dt.float8_e4m3fn_x4
ACT = mybir.ActivationFunctionType
ALU = mybir.AluOpType

P = 128
ROWS = 1024
H = 512
NACT = 128
NEXP = 8
MT = ROWS // P
HALF_MT = 4
UNITS = NEXP * 2

PE_EXPERTS = (3, 4)
Z_STEPS = {10: (6,), 11: (7,), 12: (8,), 13: (9,)}
P_STEPS = {11: (6,), 12: (7,), 13: (8,), 14: (9,)}

FLOPS = 2 * ROWS * H * H * NEXP + 2 * ROWS * H * NACT * NEXP


def tile_mspagent_pb_kernel(tc, h, gate_logit, e_w1, e_b1, e_w2, e_b2, out_0, out_1):
    nc = tc.nc
    with ExitStack() as ctx:
        keep = ctx.enter_context(tc.tile_pool(name="keep", bufs=1))
        work = ctx.enter_context(tc.tile_pool(name="work", bufs=3))
        ps_s1 = ctx.enter_context(tc.psum_pool(name="ps_s1", bufs=4))
        ps_tp = ctx.enter_context(tc.psum_pool(name="ps_tp", bufs=2))
        ps_s2 = ctx.enter_context(tc.psum_pool(name="ps_s2", bufs=2))

        with tc.manual_schedule():
            ident = keep.tile([P, P], F32, name="ident")
            make_identity(nc, ident[:])
            ones = keep.tile([P, 512], BF16, name="ones")
            nc.vector.memset(ones[:], 1.0)
            b2_row = keep.tile([P, NEXP * NACT], BF16, name="b2_row")
            nc.vector.memset(b2_row[:].bitcast(F32), 0.0)
            b1_rows = keep.tile([P, H], BF16, name="b1_rows")
            nc.vector.memset(b1_rows[:].bitcast(F32), 0.0)
            b2bc = keep.tile([P, NEXP * NACT], F32, name="b2bc")
            gate = keep.tile([P, MT * NEXP], F32, name="gate")

            gl = keep.tile([P, MT * NEXP], BF16, name="gl")

            h_view = h.rearrange("(p mt) k -> p mt k", mt=MT)
            h_sb = []
            w1_sb = []
            w2_sb = []
            for q in range(4):
                h_tile = keep.tile([P, 2, H], BF16, name="h_sb%d" % q)
                h_sb.append(h_tile)
            for ex in range(NEXP):
                for u in range(2):
                    w1_tile = keep.tile([P, 2, H], BF16, name="w1_sb%d_%d" % (ex, u))
                    w1_sb.append(w1_tile)
            for q in range(4):
                w2_tile = keep.tile([P, 2, H], BF16, name="w2_sb%d" % q)
                w2_sb.append(w2_tile)

            def load_h(q):
                nc.sync.dma_start(out=h_sb[q][:], in_=h_view[:, 2 * q:2 * q + 2, :])

            def load_w1(ex, u):
                nc.sync.dma_start(
                    out=w1_sb[2 * ex + u][:], in_=e_w1[ex].rearrange("(p t) k -> p t k", t=4)[:, 2 * u:2 * u + 2, :]
                )

            def load_w2(q):
                nc.sync.dma_start(out=w2_sb[q][:], in_=e_w2[2 * q:2 * q + 2].rearrange("x a k -> a x k"))

            for s in range(2):
                nc.sync.dma_start(out=h_sb[0][:, s, :], in_=h_view[:, s, :])
            nc.sync.dma_start(out=gl[:], in_=gate_logit.rearrange("(p mt) x -> p (mt x)", mt=MT))
            load_w1(0, 0)
            load_h(1)
            load_w1(0, 1)
            nc.sync.dma_start(out=b2_row[0:1, :], in_=e_b2.rearrange("(o x) a -> o (x a)", o=1))
            nc.sync.dma_start(out=b1_rows[0:NEXP, :], in_=e_b1)
            load_h(2)
            load_h(3)
            load_w1(1, 0)
            load_w1(1, 1)
            load_w2(0)
            load_w1(2, 0)
            load_w1(2, 1)
            load_w2(1)
            load_w1(3, 0)
            load_w1(3, 1)
            load_w2(2)
            load_w1(4, 0)
            load_w1(4, 1)
            load_w2(3)
            for ex in range(5, NEXP):
                load_w1(ex, 0)
                load_w1(ex, 1)

            nc.scalar.activation(out=gate[:], in_=gl[:], func=ACT.Sigmoid)

            def t_bank(src_tile, pool_tag, dummies):
                if pool_tag == "s1":
                    bank = ps_s1.tile([P, 2, 2, P], F32, name="tp_bank1", tag="s1")
                else:
                    bank = ps_tp.tile([P, 2, 2, P], F32, name="tp_bank", tag="tp")
                for i in range(dummies):
                    nc.tensor.matmul(
                        out=bank[:].rearrange("p s u c -> p (s u c)"), lhsT=ones[:, 0:P], rhs=ones[:], start=True, stop=True
                    )
                for s in range(2):
                    words = src_tile[:, s, :].bitcast(F32)
                    for u in range(2):
                        nc.tensor.transpose(bank[:, s, u, :], words[:, u:2 * P:2], ident[:])
                return bank

            def x_bank(bank, grouped, engine):
                dst = grouped.bitcast(F32).rearrange("p (s c u) -> p s c u", s=2, u=2)
                src = bank[:].rearrange("p s u c -> p s c u")
                if engine == "v":
                    nc.vector.tensor_copy(out=dst, in_=src)
                else:
                    nc.scalar.copy(out=dst, in_=src)

            def quantise(grouped, codes, scales):
                nc.vector.quantize_mx(out=codes.bitcast(FP8X4), scales=scales, in_=grouped)

            grp = {}
            cod = {}
            sca = {}
            for half in range(2):
                g_tile = keep.tile([P, 512 * 4], BF16, name="h_g%d" % half, align_bytes=64)
                c_tile = keep.tile([P, 512], U32, name="h_c%d" % half, align_bytes=64)
                s_tile = keep.tile([P, 512], U8, name="h_s%d" % half, align_bytes=64)
                grp[("h", half)] = g_tile
                cod[("h", half)] = c_tile
                sca[("h", half)] = s_tile
            for ex in range(NEXP):
                c_tile = keep.tile([P, 512], U32, name="w1_c%d" % ex, align_bytes=64)
                s_tile = keep.tile([P, 512], U8, name="w1_s%d" % ex, align_bytes=64)
                cod[("w1", ex)] = c_tile
                sca[("w1", ex)] = s_tile
            for q in range(4):
                c_tile = keep.tile([P, 256], U32, name="w2_c%d" % q, align_bytes=64)
                s_tile = keep.tile([P, 256], U8, name="w2_s%d" % q, align_bytes=64)
                cod[("w2", q)] = c_tile
                sca[("w2", q)] = s_tile
            live_banks = {}

            def job_t(kind, idx, b, pool_tag="tp", dummies=0):
                if kind == "w1" and b == 0:
                    g_tile = work.tile([P, 512 * 4], BF16, name="w1_g", tag="w1_g", align_bytes=64)
                    grp[(kind, idx)] = g_tile
                if kind == "w2":
                    g_tile = work.tile([P, 256 * 4], BF16, name="w2_g", tag="w2_g", bufs=2, align_bytes=64)
                    grp[(kind, idx)] = g_tile
                if kind == "h":
                    src_tile = h_sb[2 * idx + b]
                elif kind == "w1":
                    src_tile = w1_sb[2 * idx + b]
                else:
                    src_tile = w2_sb[idx]
                live_banks[(kind, idx, b)] = t_bank(src_tile, pool_tag, dummies)

            def job_x(kind, idx, b, engine):
                x_bank(live_banks[(kind, idx, b)], grp[(kind, idx)][:, b * 1024:(b + 1) * 1024], engine)

            def job_q(kind, idx, lo=0, hi=None):
                width = cod[(kind, idx)].shape[1]
                top = width if hi is None else hi
                quantise(grp[(kind, idx)][:, 4 * lo:4 * top], cod[(kind, idx)][:, lo:top], sca[(kind, idx)][:, lo:top])

            s1_banks = {}
            planes = {}
            h1_g = {}
            h1_c = {}
            h1_s = {}
            s2_bank = {}
            y_sb = {}
            z_sb = {}
            sum_bank = {}
            acc = []
            for half in range(2):
                acc_tile = keep.tile([P, HALF_MT, NACT], F32, name="acc%d" % half)
                acc.append(acc_tile)
            out1_view = out_1.rearrange("(p mt) x a -> p mt x a", mt=MT)
            out0_view = out_0.rearrange("(p mt) a -> p mt a", mt=MT)

            def mm1(n, ts=(0, 1, 2, 3), lo=0, hi=512):
                ex, half = n // 2, n % 2
                if n not in s1_banks:
                    s1_banks[n] = {}
                    pl_tile = work.tile([P, 4, 512], BF16, name="planes", tag="planes")
                    planes[n] = pl_tile
                for t in ts:
                    if lo == 0:
                        bank = ps_s1.tile([P, 512], F32, name="s1_bank", tag="s1")
                        s1_banks[n][t] = bank
                    nc.tensor.matmul_mx(
                        out=s1_banks[n][t][:, lo:hi],
                        lhsT=cod[("w1", ex)][:, t * P:(t + 1) * P].bitcast(FP8X4),
                        lhsT_scale=sca[("w1", ex)][:, t * P:(t + 1) * P],
                        rhs=cod[("h", half)][:, lo:hi].bitcast(FP8X4),
                        rhs_scale=sca[("h", half)][:, lo:hi],
                        start=True,
                        stop=True,
                    )

            def c1(n, t, lo=0, hi=512):
                ex = n // 2
                bias = b1T[:, 4 * ex + t:4 * ex + t + 1]
                nc.scalar.activation(
                    out=planes[n][:, t, lo:hi], in_=s1_banks[n][t][:, lo:hi], func=ACT.Relu, bias=bias, scale=1.0
                )

            def regroup(n, engine, lo, hi):
                if lo == hi:
                    return
                if n not in h1_g:
                    g_tile = work.tile([P, 512 * 4], BF16, name="h1_g", tag="h1_g", align_bytes=64)
                    h1_g[n] = g_tile
                dst = h1_g[n][:, 4 * lo:4 * hi].rearrange("p (c i t) -> p c t i", i=4, t=4)
                src = planes[n][:, :, lo:hi].rearrange("p t (c i) -> p c t i", i=4)
                if engine == "v":
                    nc.vector.tensor_copy(out=dst, in_=src)
                else:
                    nc.scalar.copy(out=dst, in_=src)

            def q1(n, lo=0, hi=512):
                if n not in h1_c:
                    c_tile = work.tile([P, 512], U32, name="h1_c", tag="h1_c", align_bytes=64)
                    s_tile = work.tile([P, 512], U8, name="h1_s", tag="h1_s", align_bytes=64)
                    h1_c[n] = c_tile
                    h1_s[n] = s_tile
                quantise(h1_g[n][:, 4 * lo:4 * hi], h1_c[n][:, lo:hi], h1_s[n][:, lo:hi])

            def mm2(n, tiles=(0, 1, 2, 3)):
                ex = n // 2
                bank = ps_s2.tile([P, HALF_MT, NACT], F32, name="s2_bank", tag="s2")
                lo = (ex % 2) * NACT
                for i in tiles:
                    s2_bank[(n, i)] = bank
                    nc.tensor.matmul_mx(
                        out=bank[:, i, :],
                        lhsT=h1_c[n][:, i * P:(i + 1) * P].bitcast(FP8X4),
                        lhsT_scale=h1_s[n][:, i * P:(i + 1) * P],
                        rhs=cod[("w2", ex // 2)][:, lo:lo + NACT].bitcast(FP8X4),
                        rhs_scale=sca[("w2", ex // 2)][:, lo:lo + NACT],
                        start=True,
                        stop=True,
                    )

            def add_b2(n, lo=0, hi=HALF_MT):
                ex = n // 2
                if n not in y_sb:
                    y_tile = work.tile([P, HALF_MT, NACT], F32, name="y_sb", tag="y_sb", bufs=10)
                    y_sb[n] = y_tile
                nc.vector.tensor_tensor(
                    out=y_sb[n][:, lo:hi, :],
                    in0=s2_bank[(n, lo)][:, lo:hi, :],
                    in1=b2bc[:, ex * NACT:(ex + 1) * NACT].unsqueeze(1).to_broadcast([P, hi - lo, NACT]),
                    op=ALU.add,
                )

            def gate_sum(n, lo=0, hi=HALF_MT):
                ex, half = n // 2, n % 2
                if ex in PE_EXPERTS:
                    return
                for i in range(lo, hi):
                    col = (half * HALF_MT + i) * NEXP + ex
                    if ex == 0:
                        nc.vector.tensor_scalar(
                            out=acc[half][:, i, :], in0=y_sb[n][:, i, :], scalar1=gate[:, col:col + 1], scalar2=None, op0=ALU.mult
                        )
                    else:
                        nc.vector.scalar_tensor_tensor(
                            out=acc[half][:, i, :],
                            in0=y_sb[n][:, i, :],
                            scalar=gate[:, col:col + 1],
                            in1=sum_bank[half][:, i, :] if ex == NEXP - 1 else acc[half][:, i, :],
                            op0=ALU.mult,
                            op1=ALU.add,
                        )

            def scale_by_gate(n):
                z_tile = work.tile([P, HALF_MT, NACT], F32, name="z_sb", tag="z_sb", bufs=4)
                z_sb[n] = z_tile
                for i in range(HALF_MT):
                    col = ((n % 2) * HALF_MT + i) * NEXP + n // 2
                    nc.scalar.activation(out=z_tile[:, i, :], in_=y_sb[n][:, i, :], func=ACT.Copy, scale=gate[:, col:col + 1])

            def bank_add(half, term, start, stop):
                if start:
                    bank = ps_tp.tile([P, HALF_MT, NACT], F32, name="sum_bank", tag="tp")
                    sum_bank[half] = bank
                nc.tensor.matmul(
                    out=sum_bank[half][:].rearrange("p i a -> p (i a)"),
                    lhsT=ident[:],
                    rhs=term[:].rearrange("p i a -> p (i a)"),
                    start=start,
                    stop=stop,
                )

            def store(n, lo=0, hi=HALF_MT):
                ex, half = n // 2, n % 2
                a, b = half * HALF_MT + lo, half * HALF_MT + hi
                nc.sync.dma_start(out=out1_view[:, a:b, ex, :], in_=y_sb[n][:, lo:hi, :])
                if ex == NEXP - 1:
                    nc.sync.dma_start(out=out0_view[:, a:b, :], in_=acc[half][:, lo:hi, :])

            def warm_up(count):
                warm_bank = ps_s2.tile([P, 512], F32, name="warm_bank", tag="s2")
                for i in range(count):
                    nc.tensor.matmul(out=warm_bank[:], lhsT=ones[:, 0:P], rhs=ones[:], start=True, stop=True)

            def spread_b2(c):
                b2_bank = ps_s2.tile([P, 512], F32, name="b2_bank", tag="s2")
                cols = slice(c * 512, (c + 1) * 512)
                nc.tensor.matmul(out=b2_bank[:], lhsT=ones[:, 0:P], rhs=b2_row[:, cols], start=True, stop=True)
                b2_banks[c] = b2_bank

            def exit_b2(c):
                nc.scalar.copy(out=b2bc[:, c * 512:(c + 1) * 512], in_=b2_banks[c][:])

            b2_banks = {}
            warm_up(4)
            job_t("h", 0, 0)
            job_t("w1", 0, 0, "s1")
            for c in range(2):
                spread_b2(c)
            job_t("h", 0, 1)
            job_t("w1", 0, 1, "s1")
            job_x("h", 0, 0, "v")
            job_x("w1", 0, 0, "s")
            job_q("h", 0, 0, 256)
            exit_b2(0)
            job_x("h", 0, 1, "s")
            b1_bank = ps_s2.tile([P, 512], F32, name="b1_bank", tag="s2")
            b1T = keep.tile([P, 4 * NEXP], F32, name="b1T")
            for u in range(2):
                nc.tensor.transpose(b1_bank[:, u * P:(u + 1) * P], b1_rows[:].bitcast(F32)[:, u:2 * P:2], ident[:])
            for u in range(2):
                nc.scalar.copy(
                    out=b1T[:].rearrange("p (x u e) -> p x u e", u=2, e=2)[:, :, u, :],
                    in_=b1_bank[:, u * P:(u + 1) * P].bitcast(BF16)[:, 0:2 * NEXP].rearrange("p (x e) -> p x e", e=2),
                )
            job_q("w1", 0, 0, 256)
            job_x("w1", 0, 1, "v")
            job_q("h", 0, 256, 512)
            job_q("w1", 0, 256, 512)
            mm1(0, (0, 1), 0, 256)
            job_t("h", 1, 0, dummies=1)
            for t in range(2):
                c1(0, t, 0, 256)
            exit_b2(1)
            job_t("h", 1, 1)
            mm1(0, (0, 1), 256, 512)
            mm1(0, (2, 3))
            for t in range(2):
                c1(0, t, 256, 512)
            for t in range(2, 4):
                c1(0, t)
            job_x("h", 1, 0, "v")
            job_x("h", 1, 1, "v")
            job_t("w1", 1, 0)
            job_t("w1", 1, 1)
            job_q("h", 1)
            job_x("w1", 1, 0, "v")
            job_x("w1", 1, 1, "s")

            prep_plan = {
                0: ("w1", 2, "ss"),
                1: ("w2", 1, "s"),
                2: ("w1", 3, "ss"),
                3: ("w1", 4, "ss"),
                5: ("w2", 2, "s"),
                6: ("w1", 5, "ss"),
                7: ("w1", 6, "ss"),
                9: ("w2", 3, "s"),
                10: ("w1", 7, "ss"),
            }

            nc.vector.tensor_scalar(out=gate[:], in0=gate[:], scalar1=1.0 / NEXP, scalar2=None, op0=ALU.mult)
        with tc.manual_schedule(engines={mybir.EngineType.DVE, mybir.EngineType.SP}):
            LAST = UNITS - 1
            for k in range(LAST):
                mm1(k + 1)
                if k >= 1:
                    mm2(k - 1)
                for n in P_STEPS.get(k, ()):
                    bank_add(n % 2, z_sb[n], n // 2 == PE_EXPERTS[0], False)
                if k == 14:
                    bank_add(0, acc[0], False, True)
                if k + 1 < LAST:
                    for t in range(4):
                        c1(k + 1, t)
                else:
                    for lo in (0, 256):
                        for t in range(4):
                            c1(LAST, t, lo, lo + 256)
                if k == 0:
                    job_t("w2", 0, 0)
                job = prep_plan.get(k)
                if job:
                    for b in range(len(job[2])):
                        job_t(job[0], job[1], b)
                    for b in range(len(job[2])):
                        if job[2][b] == "s":
                            job_x(job[0], job[1], b, "s")
                for n in Z_STEPS.get(k, ()):
                    scale_by_gate(n)
                regroup(k, "v", 0, 512)
                if k == 0:
                    job_q("w1", 1)
                    job_x("w2", 0, 0, "v")
                job = prep_plan.get(k - 1)
                if job:
                    job_q(job[0], job[1])
                if k >= 1:
                    add_b2(k - 1)
                q1(k)
                if k >= 1:
                    gate_sum(k - 1)
                    store(k - 1)
                else:
                    job_q("w2", 0)
                job = prep_plan.get(k)
                if job:
                    for b in range(len(job[2])):
                        if job[2][b] == "v":
                            job_x(job[0], job[1], b, "v")

            mm2(LAST - 1)
            bank_add(1, acc[1], False, True)
            regroup(LAST, "s", 256 - 192, 256)
            regroup(LAST, "s", 512 - 256, 512)
            regroup(LAST, "v", 0, 256 - 192)
            add_b2(LAST - 1)
            q1(LAST, 0, 256)
            mm2(LAST, (0, 1))
            regroup(LAST, "v", 256, 512 - 256)
            gate_sum(LAST - 1, 0, 2)
            q1(LAST, 256, 512)
            mm2(LAST, (2, 3))
            gate_sum(LAST - 1, 2, 4)
            store(LAST - 1)
            add_b2(LAST, 0, 2)
            add_b2(LAST, 2, 4)
            gate_sum(LAST, 0, 2)
            store(LAST, 0, 2)
            gate_sum(LAST, 2, 4)
            store(LAST, 2, 4)
